import numpy as np
import ml_dtypes


def mxq(x, axis, fmt="e4m3"):
    dtype, down = {"e4m3": (ml_dtypes.float8_e4m3fn, 7), "e5m2": (ml_dtypes.float8_e5m2, 14)}[fmt]
    v = np.moveaxis(np.asarray(x, np.float32).astype(ml_dtypes.bfloat16).astype(np.float64), axis, -1)
    blocks = v.reshape(v.shape[:-1] + (-1, 32))
    amax = np.abs(blocks).max(-1, keepdims=True)
    byte = np.maximum(np.where(amax > 0, np.frexp(amax)[1] - 1 + 127, 0) - down, 1)
    scale = np.exp2(byte - 127.0)
    codes = (blocks / scale).astype(np.float32).astype(dtype).astype(np.float64)
    return np.moveaxis((codes * scale).reshape(v.shape), -1, axis)


WIDE = False


def mx_kscale(k):
    if not WIDE:
        return np.ones(k)
    levels = np.array([10, -10, 5, -5, 0])
    a = np.random.permutation(np.resize(levels, k // 512 * 4)).reshape(k // 512, 4)
    idx = np.arange(k)
    return np.exp2(a[idx // 512, idx % 128 // 32])


BF16 = ml_dtypes.bfloat16


def bf(x):
    return np.asarray(x, np.float32).astype(BF16)


def f64(x):
    return np.asarray(x).astype(np.float64)


N, C, F, G = 2048, 3, 512, 256
F2 = F + F
EPS = 1e-08


def silu(v):
    return v / (1.0 + np.exp(-v))


def setup_inputs():
    s, u = mx_kscale(F), mx_kscale(F)
    w1 = np.random.standard_normal((G, F2)) / np.sqrt(F2)
    w1[:, :F] = w1[:, :F] / u
    return {"q": bf(np.random.standard_normal((N, 1, F)) * u),
            "mu": bf(np.random.standard_normal((N, C, F)) * s),
            "W_mix": bf(np.random.standard_normal((F2, F)) / np.sqrt(F) / s),
            "W1": bf(w1),
            "b1": bf(0.2 * np.random.standard_normal(G))}


def reference(q, mu, W_mix, W1, b1):
    mu_mix = mxq(f64(mu), 2, "e4m3") @ mxq(f64(W_mix), 1, "e4m3").T
    mu_V, mu_W = mu_mix[..., :F], mu_mix[..., F:]
    mu_Vn = np.sqrt(np.sum(mu_V * mu_V, axis=1, keepdims=True) + EPS)
    ctx = np.concatenate([f64(q), mu_Vn], axis=-1)
    h = silu((mxq(ctx, 2, "e4m3") @ mxq(f64(W1), 1, "e4m3").T) + f64(b1))
    mu_VW = np.sum(mu_V * mu_W, axis=1, keepdims=True)
    return h, mu_W, mu_VW

@@ -1,0 +1,392 @@
+from contextlib import ExitStack
+
+import concourse.mybir as mybir
+from concourse.masks import make_identity
+
+F32 = mybir.dt.float32
+BF16 = mybir.dt.bfloat16
+U32 = mybir.dt.uint32
+U8 = mybir.dt.uint8
+FP8X4 = mybir.dt.float8_e4m3fn_x4
+ACT = mybir.ActivationFunctionType
+ALU = mybir.AluOpType
+
+P = 128
+N_ATOMS, C, F, G = 2048, 3, 512, 256
+NT = N_ATOMS // P
+EPS = 1e-08
+FLOPS = 2 * N_ATOMS * C * (2 * F) * F + 2 * N_ATOMS * G * (2 * F)
+
+MANUAL = True
+MU_CHUNKS = [(0, 1), (1, 2), (2, 4), (4, 8), (8, 12), (12, 16)]
+Q_CHUNKS = [(0, 2), (2, 4), (4, 8), (8, 16)]
+SILU_CHUNKS = [(0, 4), (4, 8), (8, 12), (12, 14), (14, 16)]
+V_COPIES = ((3, 1), (7, 1), (11, 1), (14, 1), (14, 2), (15, 1), (15, 2))
+
+
+def tile_painnmixing_pa_t_kernel(tc, q, mu, W_mix, W1, b1, out_0, out_1, out_2):
+    nc = tc.nc
+    with ExitStack() as ctx:
+        const = ctx.enter_context(tc.tile_pool(name="const", bufs=1))
+        work = ctx.enter_context(tc.tile_pool(name="work", bufs=2))
+        psum = ctx.enter_context(tc.psum_pool(name="psum", bufs=1))
+        if MANUAL:
+            ctx.enter_context(tc.manual_schedule())
+
+        q_v = q.rearrange("(p t) o k -> p t (o k)", t=NT)
+        mu_v = mu.rearrange("(p t) c k -> p t c k", t=NT)
+        h_v = out_0.rearrange("(p t) o g -> p t (o g)", t=NT)
+        muw_v = out_1.rearrange("(p t) c f -> p t (c f)", t=NT)
+        vw_v = out_2.rearrange("(p t) o f -> p t (o f)", t=NT)
+        wm_v = W_mix.rearrange("(r p) k -> p r k", p=P)
+        w1_v = W1.rearrange("(r p) k -> p r k", p=P)
+
+        mu_sb = [const.tile([P, t1 - t0, C, F], BF16, name="mu_sb%d" % j) for j, (t0, t1) in enumerate(MU_CHUNKS)]
+        q_sb = [const.tile([P, t1 - t0, F], BF16, name="q_sb%d" % j) for j, (t0, t1) in enumerate(Q_CHUNKS)]
+        wm_sb = [const.tile([P, 4, F], BF16, name="wm_sb%d" % j) for j in range(2)]
+        w1_sb = const.tile([P, 2, 2 * F], BF16, name="w1_sb")
+        b1_bf = const.tile([P, G], BF16, name="b1_bf")
+        b1_f = const.tile([P, G], F32, name="b1_f")
+        ident_f = const.tile([P, P], F32, name="ident_f")
+        ident_b = const.tile([P, P], BF16, name="ident_b")
+        eps_t = const.tile([P, 1], F32, name="eps_t")
+        warm = const.tile([P, 1], F32, name="warm")
+        wm_g = [const.tile([P, 4, P, 4], BF16, name="wm_g%d" % j, align_bytes=64) for j in range(2)]
+        wm_codes = const.tile([P, 2 * F], U32, name="wm_codes", align_bytes=64)
+        wm_scales = const.tile([P, 2 * F], U8, name="wm_scales", align_bytes=64)
+        w1_g = const.tile([P, 2, 2, P, 4], BF16, name="w1_g", align_bytes=64)
+        w1_codes = const.tile([P, 2, G], U32, name="w1_codes", align_bytes=64)
+        w1_scales = const.tile([P, 2, G], U8, name="w1_scales", align_bytes=64)
+        hpre = const.tile([P, NT, G], F32, name="hpre")
+
+        def mu_rows(i, c):
+            for j, (t0, t1) in enumerate(MU_CHUNKS):
+                if t0 <= i < t1:
+                    return mu_sb[j][:].bitcast(F32)[:, i - t0, c, :]
+            return None
+
+        def q_rows(i):
+            for j, (t0, t1) in enumerate(Q_CHUNKS):
+                if t0 <= i < t1:
+                    return q_sb[j][:].bitcast(F32)[:, i - t0, :]
+            return None
+
+        def load_mu(j):
+            t0, t1 = MU_CHUNKS[j]
+            nc.sync.dma_start(out=mu_sb[j][:], in_=mu_v[:, t0:t1, :, :])
+
+        def load_q(j):
+            t0, t1 = Q_CHUNKS[j]
+            nc.sync.dma_start(out=q_sb[j][:], in_=q_v[:, t0:t1, :])
+
+        nc.sync.dma_start(out=wm_sb[0][:], in_=wm_v[:, 0:4, :])
+        load_mu(0)
+        load_q(0)
+        nc.sync.dma_start(out=wm_sb[1][:], in_=wm_v[:, 4:8, :])
+        load_mu(1)
+        load_mu(2)
+        load_q(1)
+        nc.sync.dma_start(out=w1_sb[:], in_=w1_v)
+        nc.sync.dma_start(out=b1_bf[:], in_=b1.partition_broadcast(P))
+        load_mu(3)
+        load_q(2)
+
+        nc.vector.memset(eps_t[:], EPS)
+        make_identity(nc, ident_f[:])
+        make_identity(nc, ident_b[:])
+        nc.scalar.activation(out=warm[:], in_=eps_t[:], func=ACT.Sqrt)
+
+        st = {}
+
+        def word_transposes(bank, sources):
+            for r, src in enumerate(sources):
+                for u in range(2):
+                    nc.tensor.transpose(bank[:, r, u, :], src[:, u * P:(u + 1) * P], ident_f[:])
+
+        def tin(i, half):
+            bank = psum.tile([P, 2, 2, P], F32, name="tin", tag="misc", bufs=2)
+            if half == 0:
+                st["g", i] = work.tile([P, 4, P, 4], BF16, name="g", tag="g", bufs=3, align_bytes=64)
+                word_transposes(bank, [mu_rows(i, 0), mu_rows(i, 1)])
+            else:
+                word_transposes(bank, [mu_rows(i, 2), q_rows(i)])
+            st["tin", i, half] = bank
+
+        def cpo(i, half, eng):
+            bank = st["tin", i, half]
+            dst = st["g", i][:].bitcast(F32)[:, 2 * half:2 * half + 2, :, :]
+            src = bank[:].rearrange("p r u a -> p r a u")
+            if eng == "v":
+                nc.vector.tensor_copy(out=dst, in_=src)
+            else:
+                nc.scalar.copy(out=dst, in_=src)
+
+        def quant(i):
+            codes = work.tile([P, 4 * P], U32, name="codes", tag="codes", bufs=5, align_bytes=64)
+            scales = work.tile([P, 4 * P], U8, name="scales", tag="scales", bufs=5, align_bytes=64)
+            nc.vector.quantize_mx(
+                out=codes[:].bitcast(FP8X4),
+                scales=scales[:],
+                in_=st["g", i][:].rearrange("p r a t -> p (r a t)"),
+            )
+            st["codes", i] = codes
+            st["scales", i] = scales
+
+        def mix_one(i, c, which):
+            codes, scales = st["codes", i], st["scales", i]
+            if which == "w":
+                dst = psum.tile([P, F], F32, name="w_ps", tag="w", bufs=2)
+                lo = F
+            else:
+                dst = psum.tile([P, F], F32, name="v_ps", tag="v", bufs=3)
+                lo = 0
+            nc.tensor.matmul_mx(
+                out=dst[:],
+                lhsT=codes[:, c * P:(c + 1) * P].bitcast(FP8X4),
+                lhsT_scale=scales[:, c * P:(c + 1) * P],
+                rhs=wm_codes[:, lo:lo + F].bitcast(FP8X4),
+                rhs_scale=wm_scales[:, lo:lo + F],
+                start=True,
+                stop=True,
+            )
+            st[which, i, c] = dst
+
+        def mix(i, c):
+            mix_one(i, c, "w")
+            mix_one(i, c, "v")
+
+        def cw(i, c):
+            if c == 0:
+                st["wout", i] = work.tile([P, C, F], F32, name="wout", tag="wout", bufs=4)
+            wout = st["wout", i]
+            if (i, c) in V_COPIES:
+                nc.vector.tensor_copy(out=wout[:, c, :], in_=st["w", i, c][:])
+            else:
+                nc.scalar.copy(out=wout[:, c, :], in_=st["w", i, c][:])
+
+        def sq(i, c):
+            sq_t = work.tile([P, F], F32, name="sq", tag="sq", bufs=7)
+            nc.scalar.activation(out=sq_t[:], in_=st["v", i, c][:], func=ACT.Square)
+            st["sq", i, c] = sq_t
+
+        def pr(i, c):
+            prod = work.tile([P, F], F32, name="prod", tag="prod", bufs=5)
+            nc.vector.tensor_tensor(out=prod[:], in0=st["v", i, c][:], in1=st["wout", i][:, c, :], op=ALU.mult)
+            st["prod", i, c] = prod
+            if c == 1:
+                acc = work.tile([P, F], F32, name="acc", tag="acc", bufs=2)
+                nc.gpsimd.tensor_tensor(out=acc[:], in0=st["prod", i, 0][:], in1=prod[:], op=ALU.add)
+                st["acc", i] = acc
+            if c == 2:
+                vw = work.tile([P, F], F32, name="vw", tag="vw", bufs=4)
+                nc.gpsimd.tensor_tensor(out=vw[:], in0=st["acc", i][:], in1=prod[:], op=ALU.add)
+                st["vw", i] = vw
+
+        def elementwise(i, c):
+            cw(i, c)
+            sq(i, c)
+            pr(i, c)
+
+        def tacc(i, c, tag):
+            if c == 0:
+                st["ss", i] = psum.tile([P, 4, P], F32, name="ss", tag=tag, bufs=(1 if tag == "ss" else 2))
+            ss = st["ss", i]
+            for t in range(4):
+                nc.tensor.matmul(
+                    out=ss[:, t, :],
+                    lhsT=st["sq", i, c][:, t * P:(t + 1) * P],
+                    rhs=ident_f[:],
+                    is_transpose=True,
+                    start=(c == 0 and t == 0),
+                    stop=(c == C - 1 and t == 3),
+                )
+
+        def srt(i):
+            vn_g = work.tile([P, P, 4], BF16, name="vn_g", tag="vn_g", bufs=2, align_bytes=64)
+            nc.scalar.activation(
+                out=vn_g[:],
+                in_=st["ss", i][:].rearrange("p t a -> p a t"),
+                func=ACT.Sqrt,
+                bias=eps_t[:, 0:1],
+                scale=1.0,
+            )
+            st["vn_g", i] = vn_g
+
+        def qvn(i):
+            vn_codes = work.tile([P, P], U32, name="vn_codes", tag="vn_codes", bufs=2, align_bytes=64)
+            vn_scales = work.tile([P, P], U8, name="vn_scales", tag="vn_scales", bufs=2, align_bytes=64)
+            nc.vector.quantize_mx(
+                out=vn_codes[:].bitcast(FP8X4),
+                scales=vn_scales[:],
+                in_=st["vn_g", i][:].rearrange("p a t -> p (a t)"),
+            )
+            st["vn_codes", i] = vn_codes
+            st["vn_scales", i] = vn_scales
+
+        def mxh(i):
+            h_ps = psum.tile([P, G], F32, name="h_ps", tag="misc", bufs=2)
+            nc.tensor.matmul_mx(
+                out=h_ps[:],
+                lhsT=st["codes", i][:, 3 * P:4 * P].bitcast(FP8X4),
+                lhsT_scale=st["scales", i][:, 3 * P:4 * P],
+                rhs=w1_codes[:, 0, :].bitcast(FP8X4),
+                rhs_scale=w1_scales[:, 0, :],
+                start=True,
+                stop=False,
+            )
+            nc.tensor.matmul_mx(
+                out=h_ps[:],
+                lhsT=st["vn_codes", i][:].bitcast(FP8X4),
+                lhsT_scale=st["vn_scales", i][:],
+                rhs=w1_codes[:, 1, :].bitcast(FP8X4),
+                rhs_scale=w1_scales[:, 1, :],
+                start=False,
+                stop=True,
+            )
+            st["h_ps", i] = h_ps
+
+        def bia(i):
+            nc.vector.tensor_tensor(out=hpre[:, i, :], in0=st["h_ps", i][:], in1=b1_f[:], op=ALU.add)
+
+        def wm_transposes(j, b):
+            wf = wm_sb[j][:].bitcast(F32)
+            bank = psum.tile([P, 2, 2, P], F32, name="wm_ps", tag="v", bufs=3)
+            word_transposes(bank, [wf[:, 2 * b, :], wf[:, 2 * b + 1, :]])
+            st["wm_ps", j, b] = bank
+
+        def wm_copy(j, b, eng):
+            dst = wm_g[j][:].bitcast(F32)[:, 2 * b:2 * b + 2, :, :]
+            src = st["wm_ps", j, b][:].rearrange("p r u a -> p r a u")
+            if eng == "v":
+                nc.vector.tensor_copy(out=dst, in_=src)
+            else:
+                nc.scalar.copy(out=dst, in_=src)
+
+        def quant_wm(j):
+            nc.vector.quantize_mx(
+                out=wm_codes[:, j * F:(j + 1) * F].bitcast(FP8X4),
+                scales=wm_scales[:, j * F:(j + 1) * F],
+                in_=wm_g[j][:].rearrange("p r a t -> p (r a t)"),
+            )
+
+        def w1_transposes(j):
+            if j == 0:
+                wf = w1_sb[:].bitcast(F32)
+                bank = psum.tile([P, 2, 2, P], F32, name="w1_ps0", tag="misc", bufs=2)
+                word_transposes(bank, [wf[:, 0, 0:2 * P], wf[:, 1, 0:2 * P]])
+            else:
+                bank = psum.tile([P, 2, 4, P], BF16, name="w1_ps1", tag="misc", bufs=2)
+                for r in range(2):
+                    for t in range(4):
+                        nc.tensor.transpose(bank[:, r, t, :], w1_sb[:, r, F + t * P:F + (t + 1) * P], ident_b[:])
+            st["w1_ps", j] = bank
+
+        def w1_copy(j):
+            if j == 0:
+                nc.vector.tensor_copy(
+                    out=w1_g[:].bitcast(F32)[:, 0, :, :, :], in_=st["w1_ps", 0][:].rearrange("p r u a -> p r a u")
+                )
+            else:
+                nc.vector.tensor_copy(out=w1_g[:, 1, :, :, :], in_=st["w1_ps", 1][:].rearrange("p r t a -> p r a t"))
+
+        def quant_w1():
+            nc.vector.tensor_copy(out=b1_f[:], in_=b1_bf[:])
+            nc.vector.quantize_mx(
+                out=w1_codes[:].rearrange("p j g -> p (j g)").bitcast(FP8X4),
+                scales=w1_scales[:].rearrange("p j g -> p (j g)"),
+                in_=w1_g[:].rearrange("p j r a t -> p (j r a t)"),
+            )
+
+        def store_w(i):
+            nc.sync.dma_start(out=muw_v[:, i, :], in_=st["wout", i][:].rearrange("p c f -> p (c f)"))
+
+        def store_vw(i):
+            nc.sync.dma_start(out=vw_v[:, i, :], in_=st["vw", i][:])
+
+        def ok(i):
+            return 0 <= i < NT
+
+        wm_transposes(0, 0)
+        wm_transposes(0, 1)
+        wm_copy(0, 0, "v")
+        wm_copy(0, 1, "s")
+        tin(0, 0)
+        tin(0, 1)
+        cpo(0, 0, "v")
+        cpo(0, 1, "s")
+        quant_wm(0)
+        quant(0)
+        wm_transposes(1, 0)
+        wm_copy(1, 0, "v")
+        wm_transposes(1, 1)
+        wm_copy(1, 1, "s")
+        for c in range(C):
+            mix_one(0, c, "v")
+        quant_wm(1)
+        sq(0, 0)
+        sq(0, 1)
+        tin(1, 0)
+        tin(1, 1)
+        cpo(1, 0, "v")
+
+        for i in range(0, NT + 2):
+            if ok(i + 1):
+                cpo(i + 1, 1, "v")
+            if ok(i - 2):
+                qvn(i - 2)
+            if i == 2:
+                quant_w1()
+            if ok(i + 1):
+                quant(i + 1)
+            if i == 0:
+                mix_one(0, 0, "w")
+                mix_one(0, 1, "w")
+                cw(0, 0)
+                pr(0, 0)
+                mix_one(0, 2, "w")
+            elif ok(i):
+                mix(i, 0)
+                mix(i, 1)
+                elementwise(i, 0)
+                mix(i, 2)
+            if ok(i - 2) and i < NT:
+                mxh(i - 2)
+                bia(i - 2)
+            if i < 2:
+                w1_transposes(i)
+                w1_copy(i)
+            if ok(i + 2):
+                tin(i + 2, 0)
+                cpo(i + 2, 0, "v")
+            if ok(i - 1):
+                for c in range(C):
+                    tacc(i - 1, c, "ss")
+            if ok(i + 2):
+                tin(i + 2, 1)
+            if i == 0:
+                cw(0, 1)
+                pr(0, 1)
+                sq(0, 2)
+                cw(0, 2)
+                pr(0, 2)
+            elif ok(i):
+                elementwise(i, 1)
+                elementwise(i, 2)
+            if ok(i - 1):
+                srt(i - 1)
+            if ok(i - 2) and i >= NT:
+                mxh(i - 2)
+                bia(i - 2)
+            if ok(i):
+                store_w(i)
+            if ok(i - 1):
+                store_vw(i - 1)
+            if i == 1:
+                load_mu(4)
+                load_q(3)
+            if i == 4:
+                load_mu(5)
+
+        for t0, t1 in SILU_CHUNKS:
+            nc.scalar.activation(out=hpre[:, t0:t1, :], in_=hpre[:, t0:t1, :], func=ACT.Silu)
+            nc.sync.dma_start(out=h_v[:, t0:t1, :], in_=hpre[:, t0:t1, :])

@@ -17,11 +17,46 @@ NT = N_ATOMS // P
 EPS = 1e-08
 FLOPS = 2 * N_ATOMS * C * (2 * F) * F + 2 * N_ATOMS * G * (2 * F)
 
-MANUAL = True
 MU_CHUNKS = [(0, 1), (1, 2), (2, 4), (4, 8), (8, 12), (12, 16)]
 Q_CHUNKS = [(0, 2), (2, 4), (4, 8), (8, 16)]
 SILU_CHUNKS = [(0, 4), (4, 8), (8, 12), (12, 14), (14, 16)]
-V_COPIES = ((3, 1), (7, 1), (11, 1), (14, 1), (14, 2), (15, 1), (15, 2))
+
+BANKS = {"vs": ("misc", 2), "w": ("w", 2), "v": ("v", 3), "tin": ("misc", 2), "h": ("misc", 2), "ss": ("ss", 1), "wm": ("v", 3), "w1": ("misc", 2)}
+
+PE_PAT = [("mixw", 0, 0), ("mixv", 0, 0), ("mixw", 0, 1), ("mixv", 0, 1), ("mixw", 0, 2), ("mixv", 0, 2), ("mxh", -2, 0),
+          ("tin", 2, 0), ("tacc", -1, 0), ("tacc", -1, 1), ("tacc", -1, 2), ("tin", 2, 1)]
+S_PAT = [("cw", 0, 0), ("sq", 0, 0), ("cw", 0, 1), ("sq", 0, 1), ("cw", 0, 2), ("sq", 0, 2), ("srt", -1, 0)]
+V_PAT = [("cpo", 1, 1), ("qvn", -2, 0), ("quant", 1, 0), ("pr", 0, 0), ("bia", -2, 0), ("cpo", 2, 0), ("pr", 0, 1), ("pr", 0, 2)]
+G_PAT = [("add", 0, 1), ("add", 0, 2)]
+SP_PAT = [("stw", 0, 0), ("stvw", -1, 0)]
+IT_LO, IT_HI = -3, NT + 4
+HEAD = {
+    "pe": [("wmt", 0, 0), ("wmt", 0, 1), ("tin", 0, 0), ("tin", 0, 1), ("wmt", 1, 0), ("wmt", 1, 1)],
+    "s": [("wmc", 0, 1), ("cpo", 0, 1), ("wmc", 1, 1)],
+    "v": [("wmc", 0, 0), ("cpo", 0, 0), ("qwm", 0, 0), ("quant", 0, 0), ("wmc", 1, 0), ("qwm", 1, 0)],
+}
+SPLICE = {
+    "pe": [(("tin", 3, 0), [("w1t", 0, 0)]), (("tin", 4, 0), [("w1t", 1, 0)]), (("tin", 5, 0), [("b1m", 0, 0)])],
+    "v": [(("cpo", 3, 0), [("w1c", 0, 0)]), (("cpo", 4, 0), [("w1c", 1, 0)]), (("cpo", 5, 0), [("b1c", 0, 0)]), (("qvn", 0, 0), [("qw1", 0, 0)])],
+}
+BANK_OVERRIDE = {}
+TAIL = {}
+LATE = ()
+S_CPO = ((0, 1),)
+V_CW = ()
+LATE_LOADS = {1: [("mu", 4), ("q", 3)], 4: [("mu", 5)]}
+
+PE_PAT = [('tin', 2, 0), ('tacc', -1, 0), ('tacc', -1, 1), ('tacc', -1, 2), ('tin', 2, 1), ('mixw', 0, 2),
+ ('mixv', 0, 2), ('mxh', -3, 0), ('mixv', 1, 0), ('mixw', 1, 0), ('mixw', 1, 1), ('mixv', 1, 1)]
+S_PAT = [('cw', 0, 0), ('sq', 0, 0), ('cw', 0, 1), ('sq', 0, 1), ('srt', -1, 0), ('cw', 0, 2), ('sq', 0, 2)]
+V_PAT = [('cw', -1, 2), ('pr', -1, 2), ('cw', 0, 1), ('cpo', 2, 0), ('cw', 0, 0), ('pr', 0, 0), ('cpo', 2, 1),
+ ('pr', 0, 1), ('quant', 2, 0), ('qvn', -2, 0), ('bia', -3, 0)]
+G_PAT = [('add', 0, 1), ('add', -1, 2)]
+V_CW = ((14, 1), (14, 2), (15, 1), (15, 2))
+HEAD = {'pe': [('wmt', 0, 0), ('tin', 0, 0), ('wmt', 0, 1), ('tin', 0, 1), ('wmt', 1, 0), ('wmt', 1, 1)],
+ 's': [('wmc', 0, 1), ('cpo', 0, 1), ('wmc', 1, 1)],
+ 'v': [('cpo', 0, 0), ('wmc', 0, 0), ('qwm', 0, 0), ('quant', 0, 0), ('wmc', 1, 0), ('qwm', 1, 0)]}
+SP_PAT = [('stw', 0, 0), ('stvw', -1, 0)]
 
 
 def tile_painnmixing_pa_t_kernel(tc, q, mu, W_mix, W1, b1, out_0, out_1, out_2):
@@ -30,8 +65,7 @@ def tile_painnmixing_pa_t_kernel(tc, q, mu, W_mix, W1, b1, out_0, out_1, out_2):
         const = ctx.enter_context(tc.tile_pool(name="const", bufs=1))
         work = ctx.enter_context(tc.tile_pool(name="work", bufs=2))
         psum = ctx.enter_context(tc.psum_pool(name="psum", bufs=1))
-        if MANUAL:
-            ctx.enter_context(tc.manual_schedule())
+        ctx.enter_context(tc.manual_schedule())
 
         q_v = q.rearrange("(p t) o k -> p t (o k)", t=NT)
         mu_v = mu.rearrange("(p t) c k -> p t c k", t=NT)
@@ -45,7 +79,8 @@ def tile_painnmixing_pa_t_kernel(tc, q, mu, W_mix, W1, b1, out_0, out_1, out_2):
         q_sb = [const.tile([P, t1 - t0, F], BF16, name="q_sb%d" % j) for j, (t0, t1) in enumerate(Q_CHUNKS)]
         wm_sb = [const.tile([P, 4, F], BF16, name="wm_sb%d" % j) for j in range(2)]
         w1_sb = const.tile([P, 2, 2 * F], BF16, name="w1_sb")
-        b1_bf = const.tile([P, G], BF16, name="b1_bf")
+        b1_row = const.tile([P, G], BF16, name="b1_row")
+        ones_b = const.tile([P, P], BF16, name="ones_b")
         b1_f = const.tile([P, G], F32, name="b1_f")
         ident_f = const.tile([P, P], F32, name="ident_f")
         ident_b = const.tile([P, P], BF16, name="ident_b")
@@ -58,6 +93,14 @@ def tile_painnmixing_pa_t_kernel(tc, q, mu, W_mix, W1, b1, out_0, out_1, out_2):
         w1_codes = const.tile([P, 2, G], U32, name="w1_codes", align_bytes=64)
         w1_scales = const.tile([P, 2, G], U8, name="w1_scales", align_bytes=64)
         hpre = const.tile([P, NT, G], F32, name="hpre")
+
+        turn = {}
+
+        def bank(kind, shape, dtype, i=-1):
+            group, bufs = BANK_OVERRIDE.get((kind, i), BANKS[kind])
+            k = turn.get(group, 0)
+            turn[group] = k + 1
+            return psum.tile(shape, dtype, name=kind + "_ps", tag="%s%d" % (group, k % bufs), bufs=1)
 
         def mu_rows(i, c):
             for j, (t0, t1) in enumerate(MU_CHUNKS):
@@ -79,6 +122,8 @@ def tile_painnmixing_pa_t_kernel(tc, q, mu, W_mix, W1, b1, out_0, out_1, out_2):
             t0, t1 = Q_CHUNKS[j]
             nc.sync.dma_start(out=q_sb[j][:], in_=q_v[:, t0:t1, :])
 
+        nc.vector.memset(b1_row[:], 0.0)
+        nc.vector.memset(ones_b[:], 1.0)
         nc.sync.dma_start(out=wm_sb[0][:], in_=wm_v[:, 0:4, :])
         load_mu(0)
         load_q(0)
@@ -87,7 +132,7 @@ def tile_painnmixing_pa_t_kernel(tc, q, mu, W_mix, W1, b1, out_0, out_1, out_2):
         load_mu(2)
         load_q(1)
         nc.sync.dma_start(out=w1_sb[:], in_=w1_v)
-        nc.sync.dma_start(out=b1_bf[:], in_=b1.partition_broadcast(P))
+        nc.sync.dma_start(out=b1_row[0:1, :], in_=b1.rearrange("(o g) -> o g", o=1))
         load_mu(3)
         load_q(2)
 
@@ -98,48 +143,43 @@ def tile_painnmixing_pa_t_kernel(tc, q, mu, W_mix, W1, b1, out_0, out_1, out_2):
 
         st = {}
 
-        def word_transposes(bank, sources):
+        def word_transposes(dst, sources):
             for r, src in enumerate(sources):
                 for u in range(2):
-                    nc.tensor.transpose(bank[:, r, u, :], src[:, u * P:(u + 1) * P], ident_f[:])
+                    nc.tensor.transpose(dst[:, r, u, :], src[:, u * P:(u + 1) * P], ident_f[:])
 
-        def tin(i, half):
-            bank = psum.tile([P, 2, 2, P], F32, name="tin", tag="misc", bufs=2)
-            if half == 0:
-                st["g", i] = work.tile([P, 4, P, 4], BF16, name="g", tag="g", bufs=3, align_bytes=64)
-                word_transposes(bank, [mu_rows(i, 0), mu_rows(i, 1)])
-            else:
-                word_transposes(bank, [mu_rows(i, 2), q_rows(i)])
-            st["tin", i, half] = bank
-
-        def cpo(i, half, eng):
-            bank = st["tin", i, half]
-            dst = st["g", i][:].bitcast(F32)[:, 2 * half:2 * half + 2, :, :]
-            src = bank[:].rearrange("p r u a -> p r a u")
+        def copy_out(eng, dst, src):
             if eng == "v":
                 nc.vector.tensor_copy(out=dst, in_=src)
             else:
                 nc.scalar.copy(out=dst, in_=src)
 
-        def quant(i):
-            codes = work.tile([P, 4 * P], U32, name="codes", tag="codes", bufs=5, align_bytes=64)
-            scales = work.tile([P, 4 * P], U8, name="scales", tag="scales", bufs=5, align_bytes=64)
-            nc.vector.quantize_mx(
-                out=codes[:].bitcast(FP8X4),
-                scales=scales[:],
-                in_=st["g", i][:].rearrange("p r a t -> p (r a t)"),
-            )
+        def op_tin(eng, i, half):
+            dst = bank("tin", [P, 2, 2, P], F32)
+            if ("g", i) not in st:
+                st["g", i] = work.tile([P, 4, P, 4], BF16, name="g", tag="g", bufs=3, align_bytes=64)
+            if half == 0:
+                word_transposes(dst, [mu_rows(i, 0), mu_rows(i, 1)])
+            else:
+                word_transposes(dst, [mu_rows(i, 2), q_rows(i)])
+            st["tin", i, half] = dst
+
+        def op_cpo(eng, i, half):
+            copy_out(eng, st["g", i][:].bitcast(F32)[:, 2 * half:2 * half + 2, :, :],
+                     st["tin", i, half][:].rearrange("p r u a -> p r a u"))
+
+        def op_quant(eng, i, a):
+            codes = work.tile([P, 4 * P], U32, name="codes", tag="codes", bufs=6, align_bytes=64)
+            scales = work.tile([P, 4 * P], U8, name="scales", tag="scales", bufs=6, align_bytes=64)
+            nc.vector.quantize_mx(out=codes[:].bitcast(FP8X4), scales=scales[:],
+                                  in_=st["g", i][:].rearrange("p r a t -> p (r a t)"))
             st["codes", i] = codes
             st["scales", i] = scales
 
         def mix_one(i, c, which):
             codes, scales = st["codes", i], st["scales", i]
-            if which == "w":
-                dst = psum.tile([P, F], F32, name="w_ps", tag="w", bufs=2)
-                lo = F
-            else:
-                dst = psum.tile([P, F], F32, name="v_ps", tag="v", bufs=3)
-                lo = 0
+            dst = bank(which, [P, F], F32, i)
+            lo = F if which == "w" else 0
             nc.tensor.matmul_mx(
                 out=dst[:],
                 lhsT=codes[:, c * P:(c + 1) * P].bitcast(FP8X4),
@@ -151,242 +191,263 @@ def tile_painnmixing_pa_t_kernel(tc, q, mu, W_mix, W1, b1, out_0, out_1, out_2):
             )
             st[which, i, c] = dst
 
-        def mix(i, c):
+        def op_mixw(eng, i, c):
             mix_one(i, c, "w")
+
+        def op_mixv(eng, i, c):
             mix_one(i, c, "v")
 
-        def cw(i, c):
-            if c == 0:
-                st["wout", i] = work.tile([P, C, F], F32, name="wout", tag="wout", bufs=4)
-            wout = st["wout", i]
-            if (i, c) in V_COPIES:
-                nc.vector.tensor_copy(out=wout[:, c, :], in_=st["w", i, c][:])
-            else:
-                nc.scalar.copy(out=wout[:, c, :], in_=st["w", i, c][:])
+        def op_mixs(eng, i, c):
+            mix_one(i, c, "vs")
 
-        def sq(i, c):
-            sq_t = work.tile([P, F], F32, name="sq", tag="sq", bufs=7)
-            nc.scalar.activation(out=sq_t[:], in_=st["v", i, c][:], func=ACT.Square)
+        def op_cw(eng, i, c):
+            if ("wout", i) not in st:
+                st["wout", i] = work.tile([P, C, F], F32, name="wout", tag="wout", bufs=4)
+            copy_out(eng, st["wout", i][:, c, :], st["w", i, c][:])
+
+        def op_sq(eng, i, c):
+            sq_t = work.tile([P, F], F32, name="sq", tag="sq", bufs=8)
+            nc.scalar.activation(out=sq_t[:], in_=st["vs" if i in LATE else "v", i, c][:], func=ACT.Square)
             st["sq", i, c] = sq_t
 
-        def pr(i, c):
-            prod = work.tile([P, F], F32, name="prod", tag="prod", bufs=5)
+        def op_pr(eng, i, c):
+            prod = work.tile([P, F], F32, name="prod", tag="prod", bufs=6)
             nc.vector.tensor_tensor(out=prod[:], in0=st["v", i, c][:], in1=st["wout", i][:, c, :], op=ALU.mult)
             st["prod", i, c] = prod
+
+        def op_add(eng, i, c):
             if c == 1:
                 acc = work.tile([P, F], F32, name="acc", tag="acc", bufs=2)
-                nc.gpsimd.tensor_tensor(out=acc[:], in0=st["prod", i, 0][:], in1=prod[:], op=ALU.add)
+                nc.gpsimd.tensor_tensor(out=acc[:], in0=st["prod", i, 0][:], in1=st["prod", i, 1][:], op=ALU.add)
                 st["acc", i] = acc
-            if c == 2:
+            else:
                 vw = work.tile([P, F], F32, name="vw", tag="vw", bufs=4)
-                nc.gpsimd.tensor_tensor(out=vw[:], in0=st["acc", i][:], in1=prod[:], op=ALU.add)
+                nc.gpsimd.tensor_tensor(out=vw[:], in0=st["acc", i][:], in1=st["prod", i, 2][:], op=ALU.add)
                 st["vw", i] = vw
 
-        def elementwise(i, c):
-            cw(i, c)
-            sq(i, c)
-            pr(i, c)
-
-        def tacc(i, c, tag):
+        def op_tacc(eng, i, c):
             if c == 0:
-                st["ss", i] = psum.tile([P, 4, P], F32, name="ss", tag=tag, bufs=(1 if tag == "ss" else 2))
+                st["ss", i] = bank("ss", [P, 4, P], F32, i)
             ss = st["ss", i]
             for t in range(4):
-                nc.tensor.matmul(
-                    out=ss[:, t, :],
-                    lhsT=st["sq", i, c][:, t * P:(t + 1) * P],
-                    rhs=ident_f[:],
-                    is_transpose=True,
-                    start=(c == 0 and t == 0),
-                    stop=(c == C - 1 and t == 3),
-                )
+                nc.tensor.matmul(out=ss[:, t, :], lhsT=st["sq", i, c][:, t * P:(t + 1) * P], rhs=ident_f[:],
+                                 is_transpose=True, start=(c == 0 and t == 0), stop=(c == C - 1 and t == 3))
 
-        def srt(i):
-            vn_g = work.tile([P, P, 4], BF16, name="vn_g", tag="vn_g", bufs=2, align_bytes=64)
-            nc.scalar.activation(
-                out=vn_g[:],
-                in_=st["ss", i][:].rearrange("p t a -> p a t"),
-                func=ACT.Sqrt,
-                bias=eps_t[:, 0:1],
-                scale=1.0,
-            )
+        def op_srt(eng, i, a):
+            vn_g = work.tile([P, P, 4], BF16, name="vn_g", tag="vn_g", bufs=3, align_bytes=64)
+            nc.scalar.activation(out=vn_g[:], in_=st["ss", i][:].rearrange("p t a -> p a t"), func=ACT.Sqrt,
+                                 bias=eps_t[:, 0:1], scale=1.0)
             st["vn_g", i] = vn_g
 
-        def qvn(i):
-            vn_codes = work.tile([P, P], U32, name="vn_codes", tag="vn_codes", bufs=2, align_bytes=64)
-            vn_scales = work.tile([P, P], U8, name="vn_scales", tag="vn_scales", bufs=2, align_bytes=64)
-            nc.vector.quantize_mx(
-                out=vn_codes[:].bitcast(FP8X4),
-                scales=vn_scales[:],
-                in_=st["vn_g", i][:].rearrange("p a t -> p (a t)"),
-            )
+        def op_qvn(eng, i, a):
+            vn_codes = work.tile([P, P], U32, name="vn_codes", tag="vn_codes", bufs=3, align_bytes=64)
+            vn_scales = work.tile([P, P], U8, name="vn_scales", tag="vn_scales", bufs=3, align_bytes=64)
+            nc.vector.quantize_mx(out=vn_codes[:].bitcast(FP8X4), scales=vn_scales[:],
+                                  in_=st["vn_g", i][:].rearrange("p a t -> p (a t)"))
             st["vn_codes", i] = vn_codes
             st["vn_scales", i] = vn_scales
 
-        def mxh(i):
-            h_ps = psum.tile([P, G], F32, name="h_ps", tag="misc", bufs=2)
-            nc.tensor.matmul_mx(
-                out=h_ps[:],
-                lhsT=st["codes", i][:, 3 * P:4 * P].bitcast(FP8X4),
-                lhsT_scale=st["scales", i][:, 3 * P:4 * P],
-                rhs=w1_codes[:, 0, :].bitcast(FP8X4),
-                rhs_scale=w1_scales[:, 0, :],
-                start=True,
-                stop=False,
-            )
-            nc.tensor.matmul_mx(
-                out=h_ps[:],
-                lhsT=st["vn_codes", i][:].bitcast(FP8X4),
-                lhsT_scale=st["vn_scales", i][:],
-                rhs=w1_codes[:, 1, :].bitcast(FP8X4),
-                rhs_scale=w1_scales[:, 1, :],
-                start=False,
-                stop=True,
-            )
+        def op_mxh(eng, i, a):
+            h_ps = bank("h", [P, G], F32, i)
+            nc.tensor.matmul_mx(out=h_ps[:], lhsT=st["codes", i][:, 3 * P:4 * P].bitcast(FP8X4),
+                                lhsT_scale=st["scales", i][:, 3 * P:4 * P], rhs=w1_codes[:, 0, :].bitcast(FP8X4),
+                                rhs_scale=w1_scales[:, 0, :], start=True, stop=False)
+            nc.tensor.matmul_mx(out=h_ps[:], lhsT=st["vn_codes", i][:].bitcast(FP8X4), lhsT_scale=st["vn_scales", i][:],
+                                rhs=w1_codes[:, 1, :].bitcast(FP8X4), rhs_scale=w1_scales[:, 1, :], start=False, stop=True)
             st["h_ps", i] = h_ps
 
-        def bia(i):
+        def op_bia(eng, i, a):
             nc.vector.tensor_tensor(out=hpre[:, i, :], in0=st["h_ps", i][:], in1=b1_f[:], op=ALU.add)
 
-        def wm_transposes(j, b):
+        def op_wmt(eng, j, b):
             wf = wm_sb[j][:].bitcast(F32)
-            bank = psum.tile([P, 2, 2, P], F32, name="wm_ps", tag="v", bufs=3)
-            word_transposes(bank, [wf[:, 2 * b, :], wf[:, 2 * b + 1, :]])
-            st["wm_ps", j, b] = bank
+            dst = bank("wm", [P, 2, 2, P], F32)
+            word_transposes(dst, [wf[:, 2 * b, :], wf[:, 2 * b + 1, :]])
+            st["wm_ps", j, b] = dst
 
-        def wm_copy(j, b, eng):
-            dst = wm_g[j][:].bitcast(F32)[:, 2 * b:2 * b + 2, :, :]
-            src = st["wm_ps", j, b][:].rearrange("p r u a -> p r a u")
-            if eng == "v":
-                nc.vector.tensor_copy(out=dst, in_=src)
-            else:
-                nc.scalar.copy(out=dst, in_=src)
+        def op_wmc(eng, j, b):
+            copy_out(eng, wm_g[j][:].bitcast(F32)[:, 2 * b:2 * b + 2, :, :],
+                     st["wm_ps", j, b][:].rearrange("p r u a -> p r a u"))
 
-        def quant_wm(j):
-            nc.vector.quantize_mx(
-                out=wm_codes[:, j * F:(j + 1) * F].bitcast(FP8X4),
-                scales=wm_scales[:, j * F:(j + 1) * F],
-                in_=wm_g[j][:].rearrange("p r a t -> p (r a t)"),
-            )
+        def op_qwm(eng, j, a):
+            nc.vector.quantize_mx(out=wm_codes[:, j * F:(j + 1) * F].bitcast(FP8X4),
+                                  scales=wm_scales[:, j * F:(j + 1) * F],
+                                  in_=wm_g[j][:].rearrange("p r a t -> p (r a t)"))
 
-        def w1_transposes(j):
+        def op_w1t(eng, j, a):
             if j == 0:
                 wf = w1_sb[:].bitcast(F32)
-                bank = psum.tile([P, 2, 2, P], F32, name="w1_ps0", tag="misc", bufs=2)
-                word_transposes(bank, [wf[:, 0, 0:2 * P], wf[:, 1, 0:2 * P]])
+                dst = bank("w1", [P, 2, 2, P], F32)
+                word_transposes(dst, [wf[:, 0, 0:2 * P], wf[:, 1, 0:2 * P]])
             else:
-                bank = psum.tile([P, 2, 4, P], BF16, name="w1_ps1", tag="misc", bufs=2)
+                dst = bank("w1", [P, 2, 4, P], BF16)
                 for r in range(2):
                     for t in range(4):
-                        nc.tensor.transpose(bank[:, r, t, :], w1_sb[:, r, F + t * P:F + (t + 1) * P], ident_b[:])
-            st["w1_ps", j] = bank
+                        nc.tensor.transpose(dst[:, r, t, :], w1_sb[:, r, F + t * P:F + (t + 1) * P], ident_b[:])
+            st["w1_ps", j] = dst
 
-        def w1_copy(j):
+        def op_w1c(eng, j, a):
             if j == 0:
-                nc.vector.tensor_copy(
-                    out=w1_g[:].bitcast(F32)[:, 0, :, :, :], in_=st["w1_ps", 0][:].rearrange("p r u a -> p r a u")
-                )
+                copy_out(eng, w1_g[:].bitcast(F32)[:, 0, :, :, :], st["w1_ps", 0][:].rearrange("p r u a -> p r a u"))
             else:
-                nc.vector.tensor_copy(out=w1_g[:, 1, :, :, :], in_=st["w1_ps", 1][:].rearrange("p r t a -> p r a t"))
+                copy_out(eng, w1_g[:, 1, :, :, :], st["w1_ps", 1][:].rearrange("p r t a -> p r a t"))
 
-        def quant_w1():
-            nc.vector.tensor_copy(out=b1_f[:], in_=b1_bf[:])
-            nc.vector.quantize_mx(
-                out=w1_codes[:].rearrange("p j g -> p (j g)").bitcast(FP8X4),
-                scales=w1_scales[:].rearrange("p j g -> p (j g)"),
-                in_=w1_g[:].rearrange("p j r a t -> p (j r a t)"),
-            )
+        def op_b1m(eng, j, a):
+            dst = bank("w1", [P, G], F32)
+            nc.tensor.matmul(out=dst[:], lhsT=ones_b[:], rhs=b1_row[:], start=True, stop=True)
+            st["b1_ps"] = dst
 
-        def store_w(i):
+        def op_b1c(eng, j, a):
+            nc.vector.tensor_copy(out=b1_f[:], in_=st["b1_ps"][:])
+
+        def op_qw1(eng, j, a):
+            nc.vector.quantize_mx(out=w1_codes[:].rearrange("p j g -> p (j g)").bitcast(FP8X4),
+                                  scales=w1_scales[:].rearrange("p j g -> p (j g)"),
+                                  in_=w1_g[:].rearrange("p j r a t -> p (j r a t)"))
+
+        def op_stw(eng, i, a):
             nc.sync.dma_start(out=muw_v[:, i, :], in_=st["wout", i][:].rearrange("p c f -> p (c f)"))
+            for kind, j in LATE_LOADS.get(i, []):
+                if kind == "mu":
+                    load_mu(j)
+                else:
+                    load_q(j)
 
-        def store_vw(i):
+        def op_stvw(eng, i, a):
             nc.sync.dma_start(out=vw_v[:, i, :], in_=st["vw", i][:])
 
-        def ok(i):
-            return 0 <= i < NT
-
-        wm_transposes(0, 0)
-        wm_transposes(0, 1)
-        wm_copy(0, 0, "v")
-        wm_copy(0, 1, "s")
-        tin(0, 0)
-        tin(0, 1)
-        cpo(0, 0, "v")
-        cpo(0, 1, "s")
-        quant_wm(0)
-        quant(0)
-        wm_transposes(1, 0)
-        wm_copy(1, 0, "v")
-        wm_transposes(1, 1)
-        wm_copy(1, 1, "s")
-        for c in range(C):
-            mix_one(0, c, "v")
-        quant_wm(1)
-        sq(0, 0)
-        sq(0, 1)
-        tin(1, 0)
-        tin(1, 1)
-        cpo(1, 0, "v")
-
-        for i in range(0, NT + 2):
-            if ok(i + 1):
-                cpo(i + 1, 1, "v")
-            if ok(i - 2):
-                qvn(i - 2)
-            if i == 2:
-                quant_w1()
-            if ok(i + 1):
-                quant(i + 1)
-            if i == 0:
-                mix_one(0, 0, "w")
-                mix_one(0, 1, "w")
-                cw(0, 0)
-                pr(0, 0)
-                mix_one(0, 2, "w")
-            elif ok(i):
-                mix(i, 0)
-                mix(i, 1)
-                elementwise(i, 0)
-                mix(i, 2)
-            if ok(i - 2) and i < NT:
-                mxh(i - 2)
-                bia(i - 2)
-            if i < 2:
-                w1_transposes(i)
-                w1_copy(i)
-            if ok(i + 2):
-                tin(i + 2, 0)
-                cpo(i + 2, 0, "v")
-            if ok(i - 1):
-                for c in range(C):
-                    tacc(i - 1, c, "ss")
-            if ok(i + 2):
-                tin(i + 2, 1)
-            if i == 0:
-                cw(0, 1)
-                pr(0, 1)
-                sq(0, 2)
-                cw(0, 2)
-                pr(0, 2)
-            elif ok(i):
-                elementwise(i, 1)
-                elementwise(i, 2)
-            if ok(i - 1):
-                srt(i - 1)
-            if ok(i - 2) and i >= NT:
-                mxh(i - 2)
-                bia(i - 2)
-            if ok(i):
-                store_w(i)
-            if ok(i - 1):
-                store_vw(i - 1)
-            if i == 1:
-                load_mu(4)
-                load_q(3)
-            if i == 4:
-                load_mu(5)
-
-        for t0, t1 in SILU_CHUNKS:
+        def op_silu(eng, t0, t1):
             nc.scalar.activation(out=hpre[:, t0:t1, :], in_=hpre[:, t0:t1, :], func=ACT.Silu)
+
+        def op_sth(eng, t0, t1):
             nc.sync.dma_start(out=h_v[:, t0:t1, :], in_=hpre[:, t0:t1, :])
+
+        OPS = {"tin": op_tin, "cpo": op_cpo, "quant": op_quant, "mixw": op_mixw, "mixv": op_mixv, "mixs": op_mixs, "cw": op_cw,
+               "sq": op_sq, "pr": op_pr, "add": op_add, "tacc": op_tacc, "srt": op_srt, "qvn": op_qvn, "mxh": op_mxh,
+               "bia": op_bia, "wmt": op_wmt, "wmc": op_wmc, "qwm": op_qwm, "w1t": op_w1t, "w1c": op_w1c, "qw1": op_qw1, "b1m": op_b1m, "b1c": op_b1c,
+               "stw": op_stw, "stvw": op_stvw, "silu": op_silu, "sth": op_sth}
+
+        def needs(op):
+            n, i, a = op
+            if n == "cpo":
+                return [("tin", i, a)]
+            if n == "quant":
+                return [("cpo", i, 0), ("cpo", i, 1)]
+            if n == "mixw":
+                return [("quant", i, 0), ("qwm", 1, 0)]
+            if n == "mixv" or n == "mixs":
+                return [("quant", i, 0), ("qwm", 0, 0)]
+            if n == "cw":
+                return [("mixw", i, a)]
+            if n == "sq":
+                return [("mixs" if i in LATE else "mixv", i, a)]
+            if n == "pr":
+                return [("cw", i, a), ("mixv", i, a)] + ([] if i in LATE else [("sq", i, a)])
+            if n == "add":
+                return [("pr", i, 0), ("pr", i, 1)] if a == 1 else [("add", i, 1), ("pr", i, 2)]
+            if n == "tacc":
+                return [("sq", i, a)] + ([("tacc", i, a - 1)] if a > 0 else [])
+            if n == "srt":
+                return [("tacc", i, 2)]
+            if n == "qvn":
+                return [("srt", i, 0)]
+            if n == "mxh":
+                return [("qvn", i, 0), ("qw1", 0, 0)]
+            if n == "bia":
+                return [("mxh", i, 0), ("b1c", 0, 0)]
+            if n == "b1c":
+                return [("b1m", 0, 0)]
+            if n == "wmc":
+                return [("wmt", i, a)]
+            if n == "qwm":
+                return [("wmc", i, 0), ("wmc", i, 1)]
+            if n == "w1c":
+                return [("w1t", i, 0)]
+            if n == "qw1":
+                return [("w1c", 0, 0), ("w1c", 1, 0)]
+            if n == "stw":
+                return [("cw", i, 0), ("cw", i, 1), ("cw", i, 2)]
+            if n == "stvw":
+                return [("add", i, 2)]
+            if n == "silu":
+                return [("bia", t, 0) for t in range(i, a)] + [("srt", NT - 1, 0)]
+            if n == "sth":
+                return [("silu", i, a)]
+            return []
+
+        def users(op):
+            n, i, a = op
+            if n == "tin":
+                return [("cpo", i, a)]
+            if n == "mixw":
+                return [("cw", i, a)]
+            if n == "mixv":
+                return [("pr", i, a)] + ([] if i in LATE else [("sq", i, a)])
+            if n == "mixs":
+                return [("sq", i, a)]
+            if n == "tacc":
+                return [("srt", i, 0)]
+            if n == "mxh":
+                return [("bia", i, 0)]
+            if n == "wmt":
+                return [("wmc", i, a)]
+            if n == "w1t":
+                return [("w1c", i, 0)]
+            if n == "b1m":
+                return [("b1c", 0, 0)]
+            return []
+
+        KIND = {"b1m": "w1", "tin": "tin", "mixw": "w", "mixv": "v", "mixs": "vs", "tacc": "ss", "mxh": "h", "wmt": "wm", "w1t": "w1"}
+
+        pats = {"pe": PE_PAT, "s": S_PAT, "v": V_PAT, "g": G_PAT, "sp": SP_PAT}
+        lists = {}
+        for eng in ("pe", "s", "v", "g", "sp"):
+            seq = list(HEAD.get(eng, []))
+            done = set(seq)
+            for other in TAIL:
+                for op in TAIL[other]:
+                    done.add(op)
+            for it in range(IT_LO, IT_HI):
+                for n, off, a in pats[eng]:
+                    op = (n, it + off, a)
+                    if not 0 <= it + off < NT or op in done:
+                        continue
+                    if n == "cpo" and ((op[1], a) in S_CPO) != (eng == "s"):
+                        continue
+                    if n == "cw" and ((op[1], a) in V_CW) != (eng == "v"):
+                        continue
+                    if n == "mixs":
+                        continue
+                    seq.append(op)
+                    done.add(op)
+            for before, extra in SPLICE.get(eng, []):
+                k = seq.index(before)
+                seq[k:k] = extra
+            lists[eng] = seq + list(TAIL.get(eng, []))
+        if not any(op[0] == "silu" for op in TAIL.get("s", [])):
+            for t0, t1 in SILU_CHUNKS:
+                lists["s"].append(("silu", t0, t1))
+                lists["sp"].append(("sth", t0, t1))
+
+        emitted = set()
+        pos = {eng: 0 for eng in lists}
+        alloc = {}
+        progress = True
+        while progress:
+            progress = False
+            for eng in ("pe", "s", "v", "g", "sp"):
+                while pos[eng] < len(lists[eng]):
+                    op = lists[eng][pos[eng]]
+                    if not all(x in emitted for x in needs(op)):
+                        break
+                    if op[0] in KIND and not (op[0] == "tacc" and op[2] > 0):
+                        tag, bufs = BANK_OVERRIDE.get((KIND[op[0]], op[1]), BANKS[KIND[op[0]]])
+                        hist = alloc.get(tag, [])
+                        if len(hist) >= bufs and not all(x in emitted for x in users(hist[-bufs])):
+                            break
+                        alloc[tag] = hist + [op]
+                    OPS[op[0]](eng, op[1], op[2])
+                    emitted.add(op)
+                    pos[eng] += 1
+                    progress = True
+        assert all(pos[eng] == len(lists[eng]) for eng in lists), "the orders cannot run"

@@ -21,7 +21,7 @@ MU_CHUNKS = [(0, 1), (1, 2), (2, 4), (4, 8), (8, 12), (12, 16)]
 Q_CHUNKS = [(0, 2), (2, 4), (4, 8), (8, 16)]
 SILU_CHUNKS = [(0, 4), (4, 8), (8, 12), (12, 14), (14, 16)]
 
-BANKS = {"vs": ("misc", 2), "w": ("w", 2), "v": ("v", 3), "tin": ("misc", 2), "h": ("misc", 2), "ss": ("ss", 1), "wm": ("v", 3), "w1": ("misc", 2)}
+BANKS = {"dmy": ("w", 2), "vs": ("misc", 2), "w": ("w", 2), "v": ("v", 3), "tin": ("misc", 2), "h": ("misc", 2), "ss": ("ss", 1), "wm": ("v", 3), "w1": ("misc", 2)}
 
 PE_PAT = [("mixw", 0, 0), ("mixv", 0, 0), ("mixw", 0, 1), ("mixv", 0, 1), ("mixw", 0, 2), ("mixv", 0, 2), ("mxh", -2, 0),
           ("tin", 2, 0), ("tacc", -1, 0), ("tacc", -1, 1), ("tacc", -1, 2), ("tin", 2, 1)]
@@ -48,15 +48,35 @@ LATE_LOADS = {1: [("mu", 4), ("q", 3)], 4: [("mu", 5)]}
 
 PE_PAT = [('tin', 2, 0), ('tacc', -1, 0), ('tacc', -1, 1), ('tacc', -1, 2), ('tin', 2, 1), ('mixw', 0, 2),
  ('mixv', 0, 2), ('mxh', -3, 0), ('mixv', 1, 0), ('mixw', 1, 0), ('mixw', 1, 1), ('mixv', 1, 1)]
-S_PAT = [('cw', 0, 0), ('sq', 0, 0), ('cw', 0, 1), ('sq', 0, 1), ('srt', -1, 0), ('cw', 0, 2), ('sq', 0, 2)]
+S_PAT = [('sq', 0, 0), ('cw', 0, 0), ('cw', 0, 1), ('sq', 0, 1), ('srt', -1, 0), ('cw', 0, 2), ('sq', 0, 2)]
 V_PAT = [('cw', -1, 2), ('pr', -1, 2), ('cw', 0, 1), ('cpo', 2, 0), ('cw', 0, 0), ('pr', 0, 0), ('cpo', 2, 1),
  ('pr', 0, 1), ('quant', 2, 0), ('qvn', -2, 0), ('bia', -3, 0)]
 G_PAT = [('add', 0, 1), ('add', -1, 2)]
 V_CW = ((14, 1), (14, 2), (15, 1), (15, 2))
-HEAD = {'pe': [('wmt', 0, 0), ('tin', 0, 0), ('wmt', 0, 1), ('tin', 0, 1), ('wmt', 1, 0), ('wmt', 1, 1)],
- 's': [('wmc', 0, 1), ('cpo', 0, 1), ('wmc', 1, 1)],
- 'v': [('cpo', 0, 0), ('wmc', 0, 0), ('qwm', 0, 0), ('quant', 0, 0), ('wmc', 1, 0), ('qwm', 1, 0)]}
+HEAD = {'pe': [('dmy', 0, 0), ('dmy', 1, 0), ('dmy', 2, 0), ('dmy', 3, 0), ('dmy', 4, 0), ('dmy', 5, 0),
+        ('dmy', 6, 0), ('dmy', 8, 0), ('dmy', 7, 0), ('wmt', 0, 0), ('wmt', 0, 1), ('tin', 0, 0),
+        ('tin', 0, 1), ('dmy', 10, 0), ('dmy', 9, 0), ('wmt', 1, 0), ('wmt', 1, 1), ('tin', 1, 0),
+        ('mixv', 0, 0), ('mixv', 0, 1), ('mixv', 0, 2), ('tin', 1, 1), ('mixw', 0, 0), ('mixw', 0, 1)],
+ 's': [('wmc', 0, 1), ('cpo', 0, 1), ('wmc', 1, 1), ('sq', 0, 0), ('sq', 0, 1), ('sq', 0, 2), ('cw', 0, 0),
+       ('cw', 0, 1), ('cw', 0, 2)],
+ 'v': [('wmc', 0, 0), ('cpo', 0, 0), ('qwm', 0, 0), ('quant', 0, 0), ('wmc', 1, 0), ('qwm', 1, 0),
+       ('cpo', 1, 0), ('cpo', 1, 1), ('quant', 1, 0)]}
 SP_PAT = [('stw', 0, 0), ('stvw', -1, 0)]
+TAIL = {'g': [('add', 13, 2), ('add', 15, 1), ('add', 14, 2), ('add', 15, 2)],
+ 'pe': [('mixv', 14, 0), ('mixw', 14, 0), ('mixw', 14, 1), ('mixv', 14, 1), ('tacc', 13, 0), ('tacc', 13, 1),
+        ('tacc', 13, 2), ('mixw', 14, 2), ('mixv', 14, 2), ('mxh', 11, 0), ('mixv', 15, 0), ('mixw', 15, 0),
+        ('mixw', 15, 1), ('mixv', 15, 1), ('tacc', 14, 0), ('tacc', 14, 1), ('tacc', 14, 2), ('mixw', 15, 2),
+        ('mixv', 15, 2), ('mxh', 12, 0), ('tacc', 15, 0), ('tacc', 15, 1), ('tacc', 15, 2), ('mxh', 13, 0),
+        ('mxh', 14, 0), ('mxh', 15, 0)],
+ 's': [('cw', 14, 0), ('sq', 14, 0), ('sq', 14, 1), ('srt', 13, 0), ('sq', 14, 2), ('sq', 15, 0),
+       ('cw', 15, 0), ('sq', 15, 1), ('srt', 14, 0), ('sq', 15, 2), ('srt', 15, 0), ('silu', 0, 4),
+       ('silu', 4, 8), ('silu', 8, 12), ('silu', 12, 14), ('silu', 14, 16)],
+ 'sp': [('stw', 13, 0), ('stvw', 12, 0), ('stw', 14, 0), ('stvw', 13, 0), ('stw', 15, 0), ('stvw', 14, 0),
+        ('stvw', 15, 0), ('sth', 0, 4), ('sth', 4, 8), ('sth', 8, 12), ('sth', 12, 14), ('sth', 14, 16)],
+ 'v': [('pr', 13, 2), ('cw', 14, 1), ('pr', 14, 0), ('cw', 14, 2), ('pr', 14, 1), ('qvn', 12, 0),
+       ('bia', 11, 0), ('pr', 14, 2), ('cw', 15, 1), ('pr', 15, 0), ('pr', 15, 1), ('qvn', 13, 0),
+       ('bia', 12, 0), ('cw', 15, 2), ('pr', 15, 2), ('bia', 13, 0), ('qvn', 14, 0), ('qvn', 15, 0),
+       ('bia', 14, 0), ('bia', 15, 0)]}
 
 
 def tile_painnmixing_pa_t_kernel(tc, q, mu, W_mix, W1, b1, out_0, out_1, out_2):
@@ -81,6 +101,7 @@ def tile_painnmixing_pa_t_kernel(tc, q, mu, W_mix, W1, b1, out_0, out_1, out_2):
         w1_sb = const.tile([P, 2, 2 * F], BF16, name="w1_sb")
         b1_row = const.tile([P, G], BF16, name="b1_row")
         ones_b = const.tile([P, P], BF16, name="ones_b")
+        zer_b = const.tile([P, F], BF16, name="zer_b")
         b1_f = const.tile([P, G], F32, name="b1_f")
         ident_f = const.tile([P, P], F32, name="ident_f")
         ident_b = const.tile([P, P], BF16, name="ident_b")
@@ -124,6 +145,7 @@ def tile_painnmixing_pa_t_kernel(tc, q, mu, W_mix, W1, b1, out_0, out_1, out_2):
 
         nc.vector.memset(b1_row[:], 0.0)
         nc.vector.memset(ones_b[:], 1.0)
+        nc.vector.memset(zer_b[:], 0.0)
         nc.sync.dma_start(out=wm_sb[0][:], in_=wm_v[:, 0:4, :])
         load_mu(0)
         load_q(0)
@@ -297,6 +319,10 @@ def tile_painnmixing_pa_t_kernel(tc, q, mu, W_mix, W1, b1, out_0, out_1, out_2):
             nc.tensor.matmul(out=dst[:], lhsT=ones_b[:], rhs=b1_row[:], start=True, stop=True)
             st["b1_ps"] = dst
 
+        def op_dmy(eng, j, a):
+            dst = bank("dmy", [P, F], F32)
+            nc.tensor.matmul(out=dst[:], lhsT=ones_b[:], rhs=zer_b[:], start=True, stop=True)
+
         def op_b1c(eng, j, a):
             nc.vector.tensor_copy(out=b1_f[:], in_=st["b1_ps"][:])
 
@@ -324,7 +350,7 @@ def tile_painnmixing_pa_t_kernel(tc, q, mu, W_mix, W1, b1, out_0, out_1, out_2):
 
         OPS = {"tin": op_tin, "cpo": op_cpo, "quant": op_quant, "mixw": op_mixw, "mixv": op_mixv, "mixs": op_mixs, "cw": op_cw,
                "sq": op_sq, "pr": op_pr, "add": op_add, "tacc": op_tacc, "srt": op_srt, "qvn": op_qvn, "mxh": op_mxh,
-               "bia": op_bia, "wmt": op_wmt, "wmc": op_wmc, "qwm": op_qwm, "w1t": op_w1t, "w1c": op_w1c, "qw1": op_qw1, "b1m": op_b1m, "b1c": op_b1c,
+               "bia": op_bia, "wmt": op_wmt, "wmc": op_wmc, "qwm": op_qwm, "w1t": op_w1t, "w1c": op_w1c, "qw1": op_qw1, "b1m": op_b1m, "b1c": op_b1c, "dmy": op_dmy,
                "stw": op_stw, "stvw": op_stvw, "silu": op_silu, "sth": op_sth}
 
         def needs(op):
@@ -397,7 +423,7 @@ def tile_painnmixing_pa_t_kernel(tc, q, mu, W_mix, W1, b1, out_0, out_1, out_2):
                 return [("b1c", 0, 0)]
             return []
 
-        KIND = {"b1m": "w1", "tin": "tin", "mixw": "w", "mixv": "v", "mixs": "vs", "tacc": "ss", "mxh": "h", "wmt": "wm", "w1t": "w1"}
+        KIND = {"b1m": "w1", "dmy": "dmy", "tin": "tin", "mixw": "w", "mixv": "v", "mixs": "vs", "tacc": "ss", "mxh": "h", "wmt": "wm", "w1t": "w1"}
 
         pats = {"pe": PE_PAT, "s": S_PAT, "v": V_PAT, "g": G_PAT, "sp": SP_PAT}
         lists = {}

@@ -12,91 +12,48 @@ ACT = mybir.ActivationFunctionType
 ALU = mybir.AluOpType
 
 P = 128
-N_ATOMS, C, F, G = 2048, 3, 512, 256
-NT = N_ATOMS // P
+ATOMS, C, F, G = 2048, 3, 512, 256
+NT = ATOMS // P
 EPS = 1e-08
-FLOPS = 2 * N_ATOMS * C * (2 * F) * F + 2 * N_ATOMS * G * (2 * F)
+FLOPS = 2 * ATOMS * C * (2 * F) * F + 2 * ATOMS * G * (2 * F)
 
-MU_CHUNKS = [(0, 1), (1, 2), (2, 4), (4, 8), (8, 12), (12, 16)]
-Q_CHUNKS = [(0, 2), (2, 4), (4, 8), (8, 16)]
-SILU_CHUNKS = [(0, 4), (4, 8), (8, 12), (12, 14), (14, 16)]
-
-BANKS = {"dmy": ("w", 2), "vs": ("misc", 2), "w": ("w", 2), "v": ("v", 3), "tin": ("misc", 2), "h": ("misc", 2), "ss": ("ss", 1), "wm": ("v", 3), "w1": ("misc", 2)}
-
-PE_PAT = [("mixw", 0, 0), ("mixv", 0, 0), ("mixw", 0, 1), ("mixv", 0, 1), ("mixw", 0, 2), ("mixv", 0, 2), ("mxh", -2, 0),
-          ("tin", 2, 0), ("tacc", -1, 0), ("tacc", -1, 1), ("tacc", -1, 2), ("tin", 2, 1)]
-S_PAT = [("cw", 0, 0), ("sq", 0, 0), ("cw", 0, 1), ("sq", 0, 1), ("cw", 0, 2), ("sq", 0, 2), ("srt", -1, 0)]
-V_PAT = [("cpo", 1, 1), ("qvn", -2, 0), ("quant", 1, 0), ("pr", 0, 0), ("bia", -2, 0), ("cpo", 2, 0), ("pr", 0, 1), ("pr", 0, 2)]
-G_PAT = [("add", 0, 1), ("add", 0, 2)]
-SP_PAT = [("stw", 0, 0), ("stvw", -1, 0)]
-IT_LO, IT_HI = -3, NT + 4
-HEAD = {
-    "pe": [("wmt", 0, 0), ("wmt", 0, 1), ("tin", 0, 0), ("tin", 0, 1), ("wmt", 1, 0), ("wmt", 1, 1)],
-    "s": [("wmc", 0, 1), ("cpo", 0, 1), ("wmc", 1, 1)],
-    "v": [("wmc", 0, 0), ("cpo", 0, 0), ("qwm", 0, 0), ("quant", 0, 0), ("wmc", 1, 0), ("qwm", 1, 0)],
+MU_LOADS = [(0, 1), (1, 2), (2, 4), (4, 8), (8, 12), (12, 16)]
+Q_LOADS = [(0, 2), (2, 4), (4, 8), (8, 16)]
+H_STORES = [(0, 4), (4, 8), (8, 12), (12, 14), (14, 16)]
+BANKS = {"w": 2, "v": 3, "misc": 2, "ss": 1}
+DEPTH = {
+    "grouped": 3,
+    "codes": 6,
+    "mu_w": 4,
+    "sq": 8,
+    "prod": 6,
+    "part": 2,
+    "mu_vw": 4,
+    "root": 3,
 }
-SPLICE = {
-    "pe": [(("tin", 3, 0), [("w1t", 0, 0)]), (("tin", 4, 0), [("w1t", 1, 0)]), (("tin", 5, 0), [("b1m", 0, 0)])],
-    "v": [(("cpo", 3, 0), [("w1c", 0, 0)]), (("cpo", 4, 0), [("w1c", 1, 0)]), (("cpo", 5, 0), [("b1c", 0, 0)]), (("qvn", 0, 0), [("qw1", 0, 0)])],
-}
-BANK_OVERRIDE = {}
-TAIL = {}
-LATE = ()
-S_CPO = ((0, 1),)
-V_CW = ()
-LATE_LOADS = {1: [("mu", 4), ("q", 3)], 4: [("mu", 5)]}
-
-PE_PAT = [('tin', 2, 0), ('tacc', -1, 0), ('tacc', -1, 1), ('tacc', -1, 2), ('tin', 2, 1), ('mixw', 0, 2),
- ('mixv', 0, 2), ('mxh', -3, 0), ('mixv', 1, 0), ('mixw', 1, 0), ('mixw', 1, 1), ('mixv', 1, 1)]
-S_PAT = [('sq', 0, 0), ('cw', 0, 0), ('cw', 0, 1), ('sq', 0, 1), ('srt', -1, 0), ('cw', 0, 2), ('sq', 0, 2)]
-V_PAT = [('cw', -1, 2), ('pr', -1, 2), ('cw', 0, 1), ('cpo', 2, 0), ('cw', 0, 0), ('pr', 0, 0), ('cpo', 2, 1),
- ('pr', 0, 1), ('quant', 2, 0), ('qvn', -2, 0), ('bia', -3, 0)]
-G_PAT = [('add', 0, 1), ('add', -1, 2)]
-V_CW = ((14, 1), (14, 2), (15, 1), (15, 2))
-HEAD = {'pe': [('dmy', 0, 0), ('dmy', 1, 0), ('dmy', 2, 0), ('dmy', 3, 0), ('dmy', 4, 0), ('dmy', 5, 0),
-        ('dmy', 6, 0), ('dmy', 8, 0), ('dmy', 7, 0), ('wmt', 0, 0), ('wmt', 0, 1), ('tin', 0, 0),
-        ('tin', 0, 1), ('dmy', 10, 0), ('dmy', 9, 0), ('wmt', 1, 0), ('wmt', 1, 1), ('tin', 1, 0),
-        ('mixv', 0, 0), ('mixv', 0, 1), ('mixv', 0, 2), ('tin', 1, 1), ('mixw', 0, 0), ('mixw', 0, 1)],
- 's': [('wmc', 0, 1), ('cpo', 0, 1), ('wmc', 1, 1), ('sq', 0, 0), ('sq', 0, 1), ('sq', 0, 2), ('cw', 0, 0),
-       ('cw', 0, 1), ('cw', 0, 2)],
- 'v': [('wmc', 0, 0), ('cpo', 0, 0), ('qwm', 0, 0), ('quant', 0, 0), ('wmc', 1, 0), ('qwm', 1, 0),
-       ('cpo', 1, 0), ('cpo', 1, 1), ('quant', 1, 0)]}
-SP_PAT = [('stw', 0, 0), ('stvw', -1, 0)]
-TAIL = {'g': [('add', 13, 2), ('add', 15, 1), ('add', 14, 2), ('add', 15, 2)],
- 'pe': [('mixv', 14, 0), ('mixw', 14, 0), ('mixw', 14, 1), ('mixv', 14, 1), ('tacc', 13, 0), ('tacc', 13, 1),
-        ('tacc', 13, 2), ('mixw', 14, 2), ('mixv', 14, 2), ('mxh', 11, 0), ('mixv', 15, 0), ('mixw', 15, 0),
-        ('mixw', 15, 1), ('mixv', 15, 1), ('tacc', 14, 0), ('tacc', 14, 1), ('tacc', 14, 2), ('mixw', 15, 2),
-        ('mixv', 15, 2), ('mxh', 12, 0), ('tacc', 15, 0), ('tacc', 15, 1), ('tacc', 15, 2), ('mxh', 13, 0),
-        ('mxh', 14, 0), ('mxh', 15, 0)],
- 's': [('cw', 14, 0), ('sq', 14, 0), ('sq', 14, 1), ('srt', 13, 0), ('sq', 14, 2), ('sq', 15, 0),
-       ('cw', 15, 0), ('sq', 15, 1), ('srt', 14, 0), ('sq', 15, 2), ('srt', 15, 0), ('silu', 0, 4),
-       ('silu', 4, 8), ('silu', 8, 12), ('silu', 12, 14), ('silu', 14, 16)],
- 'sp': [('stw', 13, 0), ('stvw', 12, 0), ('stw', 14, 0), ('stvw', 13, 0), ('stw', 15, 0), ('stvw', 14, 0),
-        ('stvw', 15, 0), ('sth', 0, 4), ('sth', 4, 8), ('sth', 8, 12), ('sth', 12, 14), ('sth', 14, 16)],
- 'v': [('pr', 13, 2), ('cw', 14, 1), ('pr', 14, 0), ('cw', 14, 2), ('pr', 14, 1), ('qvn', 12, 0),
-       ('bia', 11, 0), ('pr', 14, 2), ('cw', 15, 1), ('pr', 15, 0), ('pr', 15, 1), ('qvn', 13, 0),
-       ('bia', 12, 0), ('cw', 15, 2), ('pr', 15, 2), ('bia', 13, 0), ('qvn', 14, 0), ('qvn', 15, 0),
-       ('bia', 14, 0), ('bia', 15, 0)]}
+VECTOR_HELPS_FROM = NT - 2
+WARM_UP = 9
+WARM_UP_MORE = 2
 
 
 def tile_painnmixing_pa_t_kernel(tc, q, mu, W_mix, W1, b1, out_0, out_1, out_2):
     nc = tc.nc
     with ExitStack() as ctx:
         const = ctx.enter_context(tc.tile_pool(name="const", bufs=1))
-        work = ctx.enter_context(tc.tile_pool(name="work", bufs=2))
+        work = ctx.enter_context(tc.tile_pool(name="work", bufs=1))
         psum = ctx.enter_context(tc.psum_pool(name="psum", bufs=1))
         ctx.enter_context(tc.manual_schedule())
 
-        q_v = q.rearrange("(p t) o k -> p t (o k)", t=NT)
-        mu_v = mu.rearrange("(p t) c k -> p t c k", t=NT)
-        h_v = out_0.rearrange("(p t) o g -> p t (o g)", t=NT)
-        muw_v = out_1.rearrange("(p t) c f -> p t (c f)", t=NT)
-        vw_v = out_2.rearrange("(p t) o f -> p t (o f)", t=NT)
+        q_v = q.rearrange("(p i) o k -> p i (o k)", i=NT)
+        mu_v = mu.rearrange("(p i) c k -> p i c k", i=NT)
+        h_v = out_0.rearrange("(p i) o g -> p i (o g)", i=NT)
+        muw_v = out_1.rearrange("(p i) c f -> p i (c f)", i=NT)
+        vw_v = out_2.rearrange("(p i) o f -> p i (o f)", i=NT)
         wm_v = W_mix.rearrange("(r p) k -> p r k", p=P)
         w1_v = W1.rearrange("(r p) k -> p r k", p=P)
 
-        mu_sb = [const.tile([P, t1 - t0, C, F], BF16, name="mu_sb%d" % j) for j, (t0, t1) in enumerate(MU_CHUNKS)]
-        q_sb = [const.tile([P, t1 - t0, F], BF16, name="q_sb%d" % j) for j, (t0, t1) in enumerate(Q_CHUNKS)]
+        mu_sb = [const.tile([P, hi - lo, C, F], BF16, name="mu_sb%d" % j) for j, (lo, hi) in enumerate(MU_LOADS)]
+        q_sb = [const.tile([P, hi - lo, F], BF16, name="q_sb%d" % j) for j, (lo, hi) in enumerate(Q_LOADS)]
         wm_sb = [const.tile([P, 4, F], BF16, name="wm_sb%d" % j) for j in range(2)]
         w1_sb = const.tile([P, 2, 2 * F], BF16, name="w1_sb")
         b1_row = const.tile([P, G], BF16, name="b1_row")
@@ -115,33 +72,202 @@ def tile_painnmixing_pa_t_kernel(tc, q, mu, W_mix, W1, b1, out_0, out_1, out_2):
         w1_scales = const.tile([P, 2, G], U8, name="w1_scales", align_bytes=64)
         hpre = const.tile([P, NT, G], F32, name="hpre")
 
+        live = {}
         turn = {}
 
-        def bank(kind, shape, dtype, i=-1):
-            group, bufs = BANK_OVERRIDE.get((kind, i), BANKS[kind])
+        def bank(group, shape, dtype):
             k = turn.get(group, 0)
             turn[group] = k + 1
-            return psum.tile(shape, dtype, name=kind + "_ps", tag="%s%d" % (group, k % bufs), bufs=1)
+            return psum.tile(shape, dtype, name=group + "_ps", tag="%s%d" % (group, k % BANKS[group]), bufs=1)
 
-        def mu_rows(i, c):
-            for j, (t0, t1) in enumerate(MU_CHUNKS):
-                if t0 <= i < t1:
-                    return mu_sb[j][:].bitcast(F32)[:, i - t0, c, :]
-            return None
-
-        def q_rows(i):
-            for j, (t0, t1) in enumerate(Q_CHUNKS):
-                if t0 <= i < t1:
-                    return q_sb[j][:].bitcast(F32)[:, i - t0, :]
-            return None
+        def is_tile(i):
+            return 0 <= i < NT
 
         def load_mu(j):
-            t0, t1 = MU_CHUNKS[j]
-            nc.sync.dma_start(out=mu_sb[j][:], in_=mu_v[:, t0:t1, :, :])
+            lo, hi = MU_LOADS[j]
+            nc.sync.dma_start(out=mu_sb[j][:], in_=mu_v[:, lo:hi, :, :])
 
         def load_q(j):
-            t0, t1 = Q_CHUNKS[j]
-            nc.sync.dma_start(out=q_sb[j][:], in_=q_v[:, t0:t1, :])
+            lo, hi = Q_LOADS[j]
+            nc.sync.dma_start(out=q_sb[j][:], in_=q_v[:, lo:hi, :])
+
+        def mu_words(i, c):
+            j = [lo <= i < hi for lo, hi in MU_LOADS].index(True)
+            return mu_sb[j][:].bitcast(F32)[:, i - MU_LOADS[j][0], c, :]
+
+        def q_words(i):
+            j = [lo <= i < hi for lo, hi in Q_LOADS].index(True)
+            return q_sb[j][:].bitcast(F32)[:, i - Q_LOADS[j][0], :]
+
+        def transpose_words(dst, sources):
+            for r, src in enumerate(sources):
+                for u in range(2):
+                    nc.tensor.transpose(dst[:, r, u, :], src[:, u * P:(u + 1) * P], ident_f[:])
+
+        def regroup(engine, dst, src):
+            if engine == "vector":
+                nc.vector.tensor_copy(out=dst, in_=src.rearrange("p r u a -> p r a u"))
+            else:
+                nc.scalar.copy(out=dst, in_=src.rearrange("p r u a -> p r a u"))
+
+        def transpose_inputs(i, half):
+            if not is_tile(i):
+                return
+            dst = bank("misc", [P, 2, 2, P], F32)
+            if half == 0:
+                live["grouped", i] = work.tile([P, 4, P, 4], BF16, name="g", tag="g", bufs=DEPTH["grouped"], align_bytes=64)
+                transpose_words(dst, [mu_words(i, 0), mu_words(i, 1)])
+            else:
+                transpose_words(dst, [mu_words(i, 2), q_words(i)])
+            live["inputsT", i, half] = dst
+
+        def regroup_inputs(i, half, engine="vector"):
+            if not is_tile(i):
+                return
+            regroup(engine, live["grouped", i][:].bitcast(F32)[:, 2 * half:2 * half + 2, :, :], live["inputsT", i, half][:])
+
+        def quantise_inputs(i):
+            if not is_tile(i):
+                return
+            codes = work.tile([P, 4 * P], U32, name="codes", tag="codes", bufs=DEPTH["codes"], align_bytes=64)
+            scales = work.tile([P, 4 * P], U8, name="scales", tag="scales", bufs=DEPTH["codes"], align_bytes=64)
+            nc.vector.quantize_mx(out=codes[:].bitcast(FP8X4), scales=scales[:],
+                                  in_=live["grouped", i][:].rearrange("p r a t -> p (r a t)"))
+            live["codes", i] = codes
+            live["scales", i] = scales
+
+        def mix(i, c, part):
+            if not is_tile(i):
+                return
+            dst = bank(part, [P, F], F32)
+            first = 0 if part == "v" else F
+            nc.tensor.matmul_mx(
+                out=dst[:],
+                lhsT=live["codes", i][:, c * P:(c + 1) * P].bitcast(FP8X4),
+                lhsT_scale=live["scales", i][:, c * P:(c + 1) * P],
+                rhs=wm_codes[:, first:first + F].bitcast(FP8X4),
+                rhs_scale=wm_scales[:, first:first + F],
+                start=True,
+                stop=True,
+            )
+            live[part, i, c] = dst
+
+        def copy_mu_w(i, c):
+            if not is_tile(i):
+                return
+            if c == 0:
+                live["mu_w", i] = work.tile([P, C, F], F32, name="wout", tag="wout", bufs=DEPTH["mu_w"])
+            if i >= VECTOR_HELPS_FROM and c > 0:
+                nc.vector.tensor_copy(out=live["mu_w", i][:, c, :], in_=live["w", i, c][:])
+            else:
+                nc.scalar.copy(out=live["mu_w", i][:, c, :], in_=live["w", i, c][:])
+
+        def square(i, c):
+            if not is_tile(i):
+                return
+            sq = work.tile([P, F], F32, name="sq", tag="sq", bufs=DEPTH["sq"])
+            nc.scalar.activation(out=sq[:], in_=live["v", i, c][:], func=ACT.Square)
+            live["sq", i, c] = sq
+
+        def product(i, c):
+            if not is_tile(i):
+                return
+            prod = work.tile([P, F], F32, name="prod", tag="prod", bufs=DEPTH["prod"])
+            nc.vector.tensor_tensor(out=prod[:], in0=live["v", i, c][:], in1=live["mu_w", i][:, c, :], op=ALU.mult)
+            live["prod", i, c] = prod
+            if c == C - 1:
+                part = work.tile([P, F], F32, name="acc", tag="acc", bufs=DEPTH["part"])
+                nc.gpsimd.tensor_tensor(out=part[:], in0=live["prod", i, 0][:], in1=prod[:], op=ALU.add)
+                live["mu_vw", i] = work.tile([P, F], F32, name="vw", tag="vw", bufs=DEPTH["mu_vw"])
+                nc.gpsimd.tensor_tensor(out=live["mu_vw", i][:], in0=part[:], in1=live["prod", i, 1][:], op=ALU.add)
+
+        def sum_squares(i):
+            if not is_tile(i):
+                return
+            ss = bank("ss", [P, 4, P], F32)
+            for c in range(C):
+                for t in range(4):
+                    nc.tensor.matmul(out=ss[:, t, :], lhsT=live["sq", i, c][:, t * P:(t + 1) * P], rhs=ident_f[:],
+                                     is_transpose=True, start=(c == 0 and t == 0), stop=(c == C - 1 and t == 3))
+            live["ss", i] = ss
+
+        def root(i):
+            if not is_tile(i):
+                return
+            vn_g = work.tile([P, P, 4], BF16, name="vn_g", tag="vn_g", bufs=DEPTH["root"], align_bytes=64)
+            nc.scalar.activation(out=vn_g[:], in_=live["ss", i][:].rearrange("p t a -> p a t"), func=ACT.Sqrt,
+                                 bias=eps_t[:, 0:1], scale=1.0)
+            live["vn_g", i] = vn_g
+
+        def quantise_root(i):
+            if not is_tile(i):
+                return
+            vn_codes = work.tile([P, P], U32, name="vn_codes", tag="vn_codes", bufs=DEPTH["root"], align_bytes=64)
+            vn_scales = work.tile([P, P], U8, name="vn_scales", tag="vn_scales", bufs=DEPTH["root"], align_bytes=64)
+            nc.vector.quantize_mx(out=vn_codes[:].bitcast(FP8X4), scales=vn_scales[:],
+                                  in_=live["vn_g", i][:].rearrange("p a t -> p (a t)"))
+            live["vn_codes", i] = vn_codes
+            live["vn_scales", i] = vn_scales
+
+        def second_matmul(i):
+            if not is_tile(i):
+                return
+            h_ps = bank("misc", [P, G], F32)
+            nc.tensor.matmul_mx(out=h_ps[:], lhsT=live["codes", i][:, 3 * P:4 * P].bitcast(FP8X4),
+                                lhsT_scale=live["scales", i][:, 3 * P:4 * P], rhs=w1_codes[:, 0, :].bitcast(FP8X4),
+                                rhs_scale=w1_scales[:, 0, :], start=True, stop=False)
+            nc.tensor.matmul_mx(out=h_ps[:], lhsT=live["vn_codes", i][:].bitcast(FP8X4),
+                                lhsT_scale=live["vn_scales", i][:], rhs=w1_codes[:, 1, :].bitcast(FP8X4),
+                                rhs_scale=w1_scales[:, 1, :], start=False, stop=True)
+            nc.vector.tensor_tensor(out=hpre[:, i, :], in0=h_ps[:], in1=b1_f[:], op=ALU.add)
+
+        def store_mu_w(i):
+            if is_tile(i):
+                nc.sync.dma_start(out=muw_v[:, i, :], in_=live["mu_w", i][:].rearrange("p c f -> p (c f)"))
+
+        def store_mu_vw(i):
+            if is_tile(i):
+                nc.sync.dma_start(out=vw_v[:, i, :], in_=live["mu_vw", i][:])
+
+        def transpose_w_mix(j, b):
+            words = wm_sb[j][:].bitcast(F32)
+            dst = bank("v", [P, 2, 2, P], F32)
+            transpose_words(dst, [words[:, 2 * b, :], words[:, 2 * b + 1, :]])
+            live["wmT", j, b] = dst
+
+        def regroup_w_mix(j, b, engine):
+            regroup(engine, wm_g[j][:].bitcast(F32)[:, 2 * b:2 * b + 2, :, :], live["wmT", j, b][:])
+
+        def quantise_w_mix(j):
+            nc.vector.quantize_mx(out=wm_codes[:, j * F:(j + 1) * F].bitcast(FP8X4),
+                                  scales=wm_scales[:, j * F:(j + 1) * F],
+                                  in_=wm_g[j][:].rearrange("p r a t -> p (r a t)"))
+
+        def prepare_w1(part):
+            if part == 0:
+                words = w1_sb[:].bitcast(F32)
+                dst = bank("misc", [P, 2, 2, P], F32)
+                transpose_words(dst, [words[:, 0, 0:2 * P], words[:, 1, 0:2 * P]])
+                regroup("vector", w1_g[:].bitcast(F32)[:, 0, :, :, :], dst[:])
+            elif part == 1:
+                dst = bank("misc", [P, 2, 4, P], BF16)
+                for r in range(2):
+                    for t in range(4):
+                        nc.tensor.transpose(dst[:, r, t, :], w1_sb[:, r, F + t * P:F + (t + 1) * P], ident_b[:])
+                nc.vector.tensor_copy(out=w1_g[:, 1, :, :, :], in_=dst[:].rearrange("p r t a -> p r a t"))
+            else:
+                dst = bank("misc", [P, G], F32)
+                nc.tensor.matmul(out=dst[:], lhsT=ones_b[:], rhs=b1_row[:], start=True, stop=True)
+                nc.vector.tensor_copy(out=b1_f[:], in_=dst[:])
+
+        def quantise_w1():
+            nc.vector.quantize_mx(out=w1_codes[:].rearrange("p j g -> p (j g)").bitcast(FP8X4),
+                                  scales=w1_scales[:].rearrange("p j g -> p (j g)"),
+                                  in_=w1_g[:].rearrange("p j r a t -> p (j r a t)"))
+
+        def warm_up(n):
+            for k in range(n):
+                nc.tensor.matmul(out=bank("w", [P, F], F32)[:], lhsT=ones_b[:], rhs=zer_b[:], start=True, stop=True)
 
         nc.vector.memset(b1_row[:], 0.0)
         nc.vector.memset(ones_b[:], 1.0)
@@ -157,323 +283,83 @@ def tile_painnmixing_pa_t_kernel(tc, q, mu, W_mix, W1, b1, out_0, out_1, out_2):
         nc.sync.dma_start(out=b1_row[0:1, :], in_=b1.rearrange("(o g) -> o g", o=1))
         load_mu(3)
         load_q(2)
-
         nc.vector.memset(eps_t[:], EPS)
         make_identity(nc, ident_f[:])
         make_identity(nc, ident_b[:])
         nc.scalar.activation(out=warm[:], in_=eps_t[:], func=ACT.Sqrt)
 
-        st = {}
+        warm_up(WARM_UP)
+        for b in range(2):
+            transpose_w_mix(0, b)
+        regroup_w_mix(0, 0, "vector")
+        regroup_w_mix(0, 1, "scalar")
+        for half in range(2):
+            transpose_inputs(0, half)
+        regroup_inputs(0, 0, "vector")
+        regroup_inputs(0, 1, "scalar")
+        warm_up(WARM_UP_MORE)
+        quantise_w_mix(0)
+        quantise_inputs(0)
+        for b in range(2):
+            transpose_w_mix(1, b)
+        regroup_w_mix(1, 0, "vector")
+        regroup_w_mix(1, 1, "scalar")
+        quantise_w_mix(1)
+        transpose_inputs(1, 0)
+        for c in range(C):
+            mix(0, c, "v")
+        transpose_inputs(1, 1)
+        for c in range(C):
+            square(0, c)
+        mix(0, 0, "w")
+        mix(0, 1, "w")
+        regroup_inputs(1, 0)
+        regroup_inputs(1, 1)
+        quantise_inputs(1)
+        copy_mu_w(0, 0)
+        copy_mu_w(0, 1)
 
-        def word_transposes(dst, sources):
-            for r, src in enumerate(sources):
-                for u in range(2):
-                    nc.tensor.transpose(dst[:, r, u, :], src[:, u * P:(u + 1) * P], ident_f[:])
+        for i in range(NT + 3):
+            product(i - 1, 2)
+            if 1 <= i <= 3:
+                prepare_w1(i - 1)
+            transpose_inputs(i + 2, 0)
+            regroup_inputs(i + 2, 0)
+            sum_squares(i - 1)
+            transpose_inputs(i + 2, 1)
+            if i > 0:
+                square(i, 0)
+                copy_mu_w(i, 0)
+            product(i, 0)
+            regroup_inputs(i + 2, 1)
+            if i > 0:
+                copy_mu_w(i, 1)
+                square(i, 1)
+            product(i, 1)
+            root(i - 1)
+            mix(i, 2, "w")
+            if i > 0:
+                mix(i, 2, "v")
+            second_matmul(i - 3)
+            quantise_inputs(i + 2)
+            if i == 2:
+                quantise_w1()
+            quantise_root(i - 2)
+            mix(i + 1, 0, "v")
+            mix(i + 1, 0, "w")
+            copy_mu_w(i, 2)
+            if i > 0:
+                square(i, 2)
+            mix(i + 1, 1, "w")
+            mix(i + 1, 1, "v")
+            store_mu_w(i)
+            if i == 1:
+                load_mu(4)
+                load_q(3)
+            if i == 4:
+                load_mu(5)
+            store_mu_vw(i - 1)
 
-        def copy_out(eng, dst, src):
-            if eng == "v":
-                nc.vector.tensor_copy(out=dst, in_=src)
-            else:
-                nc.scalar.copy(out=dst, in_=src)
-
-        def op_tin(eng, i, half):
-            dst = bank("tin", [P, 2, 2, P], F32)
-            if ("g", i) not in st:
-                st["g", i] = work.tile([P, 4, P, 4], BF16, name="g", tag="g", bufs=3, align_bytes=64)
-            if half == 0:
-                word_transposes(dst, [mu_rows(i, 0), mu_rows(i, 1)])
-            else:
-                word_transposes(dst, [mu_rows(i, 2), q_rows(i)])
-            st["tin", i, half] = dst
-
-        def op_cpo(eng, i, half):
-            copy_out(eng, st["g", i][:].bitcast(F32)[:, 2 * half:2 * half + 2, :, :],
-                     st["tin", i, half][:].rearrange("p r u a -> p r a u"))
-
-        def op_quant(eng, i, a):
-            codes = work.tile([P, 4 * P], U32, name="codes", tag="codes", bufs=6, align_bytes=64)
-            scales = work.tile([P, 4 * P], U8, name="scales", tag="scales", bufs=6, align_bytes=64)
-            nc.vector.quantize_mx(out=codes[:].bitcast(FP8X4), scales=scales[:],
-                                  in_=st["g", i][:].rearrange("p r a t -> p (r a t)"))
-            st["codes", i] = codes
-            st["scales", i] = scales
-
-        def mix_one(i, c, which):
-            codes, scales = st["codes", i], st["scales", i]
-            dst = bank(which, [P, F], F32, i)
-            lo = F if which == "w" else 0
-            nc.tensor.matmul_mx(
-                out=dst[:],
-                lhsT=codes[:, c * P:(c + 1) * P].bitcast(FP8X4),
-                lhsT_scale=scales[:, c * P:(c + 1) * P],
-                rhs=wm_codes[:, lo:lo + F].bitcast(FP8X4),
-                rhs_scale=wm_scales[:, lo:lo + F],
-                start=True,
-                stop=True,
-            )
-            st[which, i, c] = dst
-
-        def op_mixw(eng, i, c):
-            mix_one(i, c, "w")
-
-        def op_mixv(eng, i, c):
-            mix_one(i, c, "v")
-
-        def op_mixs(eng, i, c):
-            mix_one(i, c, "vs")
-
-        def op_cw(eng, i, c):
-            if ("wout", i) not in st:
-                st["wout", i] = work.tile([P, C, F], F32, name="wout", tag="wout", bufs=4)
-            copy_out(eng, st["wout", i][:, c, :], st["w", i, c][:])
-
-        def op_sq(eng, i, c):
-            sq_t = work.tile([P, F], F32, name="sq", tag="sq", bufs=8)
-            nc.scalar.activation(out=sq_t[:], in_=st["vs" if i in LATE else "v", i, c][:], func=ACT.Square)
-            st["sq", i, c] = sq_t
-
-        def op_pr(eng, i, c):
-            prod = work.tile([P, F], F32, name="prod", tag="prod", bufs=6)
-            nc.vector.tensor_tensor(out=prod[:], in0=st["v", i, c][:], in1=st["wout", i][:, c, :], op=ALU.mult)
-            st["prod", i, c] = prod
-
-        def op_add(eng, i, c):
-            if c == 1:
-                acc = work.tile([P, F], F32, name="acc", tag="acc", bufs=2)
-                nc.gpsimd.tensor_tensor(out=acc[:], in0=st["prod", i, 0][:], in1=st["prod", i, 1][:], op=ALU.add)
-                st["acc", i] = acc
-            else:
-                vw = work.tile([P, F], F32, name="vw", tag="vw", bufs=4)
-                nc.gpsimd.tensor_tensor(out=vw[:], in0=st["acc", i][:], in1=st["prod", i, 2][:], op=ALU.add)
-                st["vw", i] = vw
-
-        def op_tacc(eng, i, c):
-            if c == 0:
-                st["ss", i] = bank("ss", [P, 4, P], F32, i)
-            ss = st["ss", i]
-            for t in range(4):
-                nc.tensor.matmul(out=ss[:, t, :], lhsT=st["sq", i, c][:, t * P:(t + 1) * P], rhs=ident_f[:],
-                                 is_transpose=True, start=(c == 0 and t == 0), stop=(c == C - 1 and t == 3))
-
-        def op_srt(eng, i, a):
-            vn_g = work.tile([P, P, 4], BF16, name="vn_g", tag="vn_g", bufs=3, align_bytes=64)
-            nc.scalar.activation(out=vn_g[:], in_=st["ss", i][:].rearrange("p t a -> p a t"), func=ACT.Sqrt,
-                                 bias=eps_t[:, 0:1], scale=1.0)
-            st["vn_g", i] = vn_g
-
-        def op_qvn(eng, i, a):
-            vn_codes = work.tile([P, P], U32, name="vn_codes", tag="vn_codes", bufs=3, align_bytes=64)
-            vn_scales = work.tile([P, P], U8, name="vn_scales", tag="vn_scales", bufs=3, align_bytes=64)
-            nc.vector.quantize_mx(out=vn_codes[:].bitcast(FP8X4), scales=vn_scales[:],
-                                  in_=st["vn_g", i][:].rearrange("p a t -> p (a t)"))
-            st["vn_codes", i] = vn_codes
-            st["vn_scales", i] = vn_scales
-
-        def op_mxh(eng, i, a):
-            h_ps = bank("h", [P, G], F32, i)
-            nc.tensor.matmul_mx(out=h_ps[:], lhsT=st["codes", i][:, 3 * P:4 * P].bitcast(FP8X4),
-                                lhsT_scale=st["scales", i][:, 3 * P:4 * P], rhs=w1_codes[:, 0, :].bitcast(FP8X4),
-                                rhs_scale=w1_scales[:, 0, :], start=True, stop=False)
-            nc.tensor.matmul_mx(out=h_ps[:], lhsT=st["vn_codes", i][:].bitcast(FP8X4), lhsT_scale=st["vn_scales", i][:],
-                                rhs=w1_codes[:, 1, :].bitcast(FP8X4), rhs_scale=w1_scales[:, 1, :], start=False, stop=True)
-            st["h_ps", i] = h_ps
-
-        def op_bia(eng, i, a):
-            nc.vector.tensor_tensor(out=hpre[:, i, :], in0=st["h_ps", i][:], in1=b1_f[:], op=ALU.add)
-
-        def op_wmt(eng, j, b):
-            wf = wm_sb[j][:].bitcast(F32)
-            dst = bank("wm", [P, 2, 2, P], F32)
-            word_transposes(dst, [wf[:, 2 * b, :], wf[:, 2 * b + 1, :]])
-            st["wm_ps", j, b] = dst
-
-        def op_wmc(eng, j, b):
-            copy_out(eng, wm_g[j][:].bitcast(F32)[:, 2 * b:2 * b + 2, :, :],
-                     st["wm_ps", j, b][:].rearrange("p r u a -> p r a u"))
-
-        def op_qwm(eng, j, a):
-            nc.vector.quantize_mx(out=wm_codes[:, j * F:(j + 1) * F].bitcast(FP8X4),
-                                  scales=wm_scales[:, j * F:(j + 1) * F],
-                                  in_=wm_g[j][:].rearrange("p r a t -> p (r a t)"))
-
-        def op_w1t(eng, j, a):
-            if j == 0:
-                wf = w1_sb[:].bitcast(F32)
-                dst = bank("w1", [P, 2, 2, P], F32)
-                word_transposes(dst, [wf[:, 0, 0:2 * P], wf[:, 1, 0:2 * P]])
-            else:
-                dst = bank("w1", [P, 2, 4, P], BF16)
-                for r in range(2):
-                    for t in range(4):
-                        nc.tensor.transpose(dst[:, r, t, :], w1_sb[:, r, F + t * P:F + (t + 1) * P], ident_b[:])
-            st["w1_ps", j] = dst
-
-        def op_w1c(eng, j, a):
-            if j == 0:
-                copy_out(eng, w1_g[:].bitcast(F32)[:, 0, :, :, :], st["w1_ps", 0][:].rearrange("p r u a -> p r a u"))
-            else:
-                copy_out(eng, w1_g[:, 1, :, :, :], st["w1_ps", 1][:].rearrange("p r t a -> p r a t"))
-
-        def op_b1m(eng, j, a):
-            dst = bank("w1", [P, G], F32)
-            nc.tensor.matmul(out=dst[:], lhsT=ones_b[:], rhs=b1_row[:], start=True, stop=True)
-            st["b1_ps"] = dst
-
-        def op_dmy(eng, j, a):
-            dst = bank("dmy", [P, F], F32)
-            nc.tensor.matmul(out=dst[:], lhsT=ones_b[:], rhs=zer_b[:], start=True, stop=True)
-
-        def op_b1c(eng, j, a):
-            nc.vector.tensor_copy(out=b1_f[:], in_=st["b1_ps"][:])
-
-        def op_qw1(eng, j, a):
-            nc.vector.quantize_mx(out=w1_codes[:].rearrange("p j g -> p (j g)").bitcast(FP8X4),
-                                  scales=w1_scales[:].rearrange("p j g -> p (j g)"),
-                                  in_=w1_g[:].rearrange("p j r a t -> p (j r a t)"))
-
-        def op_stw(eng, i, a):
-            nc.sync.dma_start(out=muw_v[:, i, :], in_=st["wout", i][:].rearrange("p c f -> p (c f)"))
-            for kind, j in LATE_LOADS.get(i, []):
-                if kind == "mu":
-                    load_mu(j)
-                else:
-                    load_q(j)
-
-        def op_stvw(eng, i, a):
-            nc.sync.dma_start(out=vw_v[:, i, :], in_=st["vw", i][:])
-
-        def op_silu(eng, t0, t1):
-            nc.scalar.activation(out=hpre[:, t0:t1, :], in_=hpre[:, t0:t1, :], func=ACT.Silu)
-
-        def op_sth(eng, t0, t1):
-            nc.sync.dma_start(out=h_v[:, t0:t1, :], in_=hpre[:, t0:t1, :])
-
-        OPS = {"tin": op_tin, "cpo": op_cpo, "quant": op_quant, "mixw": op_mixw, "mixv": op_mixv, "mixs": op_mixs, "cw": op_cw,
-               "sq": op_sq, "pr": op_pr, "add": op_add, "tacc": op_tacc, "srt": op_srt, "qvn": op_qvn, "mxh": op_mxh,
-               "bia": op_bia, "wmt": op_wmt, "wmc": op_wmc, "qwm": op_qwm, "w1t": op_w1t, "w1c": op_w1c, "qw1": op_qw1, "b1m": op_b1m, "b1c": op_b1c, "dmy": op_dmy,
-               "stw": op_stw, "stvw": op_stvw, "silu": op_silu, "sth": op_sth}
-
-        def needs(op):
-            n, i, a = op
-            if n == "cpo":
-                return [("tin", i, a)]
-            if n == "quant":
-                return [("cpo", i, 0), ("cpo", i, 1)]
-            if n == "mixw":
-                return [("quant", i, 0), ("qwm", 1, 0)]
-            if n == "mixv" or n == "mixs":
-                return [("quant", i, 0), ("qwm", 0, 0)]
-            if n == "cw":
-                return [("mixw", i, a)]
-            if n == "sq":
-                return [("mixs" if i in LATE else "mixv", i, a)]
-            if n == "pr":
-                return [("cw", i, a), ("mixv", i, a)] + ([] if i in LATE else [("sq", i, a)])
-            if n == "add":
-                return [("pr", i, 0), ("pr", i, 1)] if a == 1 else [("add", i, 1), ("pr", i, 2)]
-            if n == "tacc":
-                return [("sq", i, a)] + ([("tacc", i, a - 1)] if a > 0 else [])
-            if n == "srt":
-                return [("tacc", i, 2)]
-            if n == "qvn":
-                return [("srt", i, 0)]
-            if n == "mxh":
-                return [("qvn", i, 0), ("qw1", 0, 0)]
-            if n == "bia":
-                return [("mxh", i, 0), ("b1c", 0, 0)]
-            if n == "b1c":
-                return [("b1m", 0, 0)]
-            if n == "wmc":
-                return [("wmt", i, a)]
-            if n == "qwm":
-                return [("wmc", i, 0), ("wmc", i, 1)]
-            if n == "w1c":
-                return [("w1t", i, 0)]
-            if n == "qw1":
-                return [("w1c", 0, 0), ("w1c", 1, 0)]
-            if n == "stw":
-                return [("cw", i, 0), ("cw", i, 1), ("cw", i, 2)]
-            if n == "stvw":
-                return [("add", i, 2)]
-            if n == "silu":
-                return [("bia", t, 0) for t in range(i, a)] + [("srt", NT - 1, 0)]
-            if n == "sth":
-                return [("silu", i, a)]
-            return []
-
-        def users(op):
-            n, i, a = op
-            if n == "tin":
-                return [("cpo", i, a)]
-            if n == "mixw":
-                return [("cw", i, a)]
-            if n == "mixv":
-                return [("pr", i, a)] + ([] if i in LATE else [("sq", i, a)])
-            if n == "mixs":
-                return [("sq", i, a)]
-            if n == "tacc":
-                return [("srt", i, 0)]
-            if n == "mxh":
-                return [("bia", i, 0)]
-            if n == "wmt":
-                return [("wmc", i, a)]
-            if n == "w1t":
-                return [("w1c", i, 0)]
-            if n == "b1m":
-                return [("b1c", 0, 0)]
-            return []
-
-        KIND = {"b1m": "w1", "dmy": "dmy", "tin": "tin", "mixw": "w", "mixv": "v", "mixs": "vs", "tacc": "ss", "mxh": "h", "wmt": "wm", "w1t": "w1"}
-
-        pats = {"pe": PE_PAT, "s": S_PAT, "v": V_PAT, "g": G_PAT, "sp": SP_PAT}
-        lists = {}
-        for eng in ("pe", "s", "v", "g", "sp"):
-            seq = list(HEAD.get(eng, []))
-            done = set(seq)
-            for other in TAIL:
-                for op in TAIL[other]:
-                    done.add(op)
-            for it in range(IT_LO, IT_HI):
-                for n, off, a in pats[eng]:
-                    op = (n, it + off, a)
-                    if not 0 <= it + off < NT or op in done:
-                        continue
-                    if n == "cpo" and ((op[1], a) in S_CPO) != (eng == "s"):
-                        continue
-                    if n == "cw" and ((op[1], a) in V_CW) != (eng == "v"):
-                        continue
-                    if n == "mixs":
-                        continue
-                    seq.append(op)
-                    done.add(op)
-            for before, extra in SPLICE.get(eng, []):
-                k = seq.index(before)
-                seq[k:k] = extra
-            lists[eng] = seq + list(TAIL.get(eng, []))
-        if not any(op[0] == "silu" for op in TAIL.get("s", [])):
-            for t0, t1 in SILU_CHUNKS:
-                lists["s"].append(("silu", t0, t1))
-                lists["sp"].append(("sth", t0, t1))
-
-        emitted = set()
-        pos = {eng: 0 for eng in lists}
-        alloc = {}
-        progress = True
-        while progress:
-            progress = False
-            for eng in ("pe", "s", "v", "g", "sp"):
-                while pos[eng] < len(lists[eng]):
-                    op = lists[eng][pos[eng]]
-                    if not all(x in emitted for x in needs(op)):
-                        break
-                    if op[0] in KIND and not (op[0] == "tacc" and op[2] > 0):
-                        tag, bufs = BANK_OVERRIDE.get((KIND[op[0]], op[1]), BANKS[KIND[op[0]]])
-                        hist = alloc.get(tag, [])
-                        if len(hist) >= bufs and not all(x in emitted for x in users(hist[-bufs])):
-                            break
-                        alloc[tag] = hist + [op]
-                    OPS[op[0]](eng, op[1], op[2])
-                    emitted.add(op)
-                    pos[eng] += 1
-                    progress = True
-        assert all(pos[eng] == len(lists[eng]) for eng in lists), "the orders cannot run"
+        for lo, hi in H_STORES:
+            nc.scalar.activation(out=hpre[:, lo:hi, :], in_=hpre[:, lo:hi, :], func=ACT.Silu)
+            nc.sync.dma_start(out=h_v[:, lo:hi, :], in_=hpre[:, lo:hi, :])

@@ -27,7 +27,7 @@ DEPTH = {
     "mu_w": 4,
     "sq": 8,
     "prod": 6,
-    "part": 2,
+    "sum01": 2,
     "mu_vw": 4,
     "root": 3,
 }
@@ -63,7 +63,7 @@ def tile_painnmixing_pa_t_kernel(tc, q, mu, W_mix, W1, b1, out_0, out_1, out_2):
         ident_f = const.tile([P, P], F32, name="ident_f")
         ident_b = const.tile([P, P], BF16, name="ident_b")
         eps_t = const.tile([P, 1], F32, name="eps_t")
-        warm = const.tile([P, 1], F32, name="warm")
+        first_root = const.tile([P, 1], F32, name="first_root")
         wm_g = [const.tile([P, 4, P, 4], BF16, name="wm_g%d" % j, align_bytes=64) for j in range(2)]
         wm_codes = const.tile([P, 2 * F], U32, name="wm_codes", align_bytes=64)
         wm_scales = const.tile([P, 2 * F], U8, name="wm_scales", align_bytes=64)
@@ -175,11 +175,18 @@ def tile_painnmixing_pa_t_kernel(tc, q, mu, W_mix, W1, b1, out_0, out_1, out_2):
             prod = work.tile([P, F], F32, name="prod", tag="prod", bufs=DEPTH["prod"])
             nc.vector.tensor_tensor(out=prod[:], in0=live["v", i, c][:], in1=live["mu_w", i][:, c, :], op=ALU.mult)
             live["prod", i, c] = prod
-            if c == C - 1:
-                part = work.tile([P, F], F32, name="acc", tag="acc", bufs=DEPTH["part"])
-                nc.gpsimd.tensor_tensor(out=part[:], in0=live["prod", i, 0][:], in1=prod[:], op=ALU.add)
-                live["mu_vw", i] = work.tile([P, F], F32, name="vw", tag="vw", bufs=DEPTH["mu_vw"])
-                nc.gpsimd.tensor_tensor(out=live["mu_vw", i][:], in0=part[:], in1=live["prod", i, 1][:], op=ALU.add)
+
+        def add_first_two_products(i):
+            if not is_tile(i):
+                return
+            live["sum01", i] = work.tile([P, F], F32, name="acc", tag="acc", bufs=DEPTH["sum01"])
+            nc.gpsimd.tensor_tensor(out=live["sum01", i][:], in0=live["prod", i, 0][:], in1=live["prod", i, 1][:], op=ALU.add)
+
+        def add_third_product(i):
+            if not is_tile(i):
+                return
+            live["mu_vw", i] = work.tile([P, F], F32, name="vw", tag="vw", bufs=DEPTH["mu_vw"])
+            nc.gpsimd.tensor_tensor(out=live["mu_vw", i][:], in0=live["sum01", i][:], in1=live["prod", i, 2][:], op=ALU.add)
 
         def sum_squares(i):
             if not is_tile(i):
@@ -286,7 +293,7 @@ def tile_painnmixing_pa_t_kernel(tc, q, mu, W_mix, W1, b1, out_0, out_1, out_2):
         nc.vector.memset(eps_t[:], EPS)
         make_identity(nc, ident_f[:])
         make_identity(nc, ident_b[:])
-        nc.scalar.activation(out=warm[:], in_=eps_t[:], func=ACT.Sqrt)
+        nc.scalar.activation(out=first_root[:], in_=eps_t[:], func=ACT.Sqrt)
 
         warm_up(WARM_UP)
         for b in range(2):
@@ -336,15 +343,17 @@ def tile_painnmixing_pa_t_kernel(tc, q, mu, W_mix, W1, b1, out_0, out_1, out_2):
                 copy_mu_w(i, 1)
                 square(i, 1)
             product(i, 1)
+            add_first_two_products(i)
+            add_third_product(i - 1)
+            quantise_inputs(i + 2)
+            if i == 2:
+                quantise_w1()
+            quantise_root(i - 2)
             root(i - 1)
             mix(i, 2, "w")
             if i > 0:
                 mix(i, 2, "v")
             second_matmul(i - 3)
-            quantise_inputs(i + 2)
-            if i == 2:
-                quantise_w1()
-            quantise_root(i - 2)
             mix(i + 1, 0, "v")
             mix(i + 1, 0, "w")
             copy_mu_w(i, 2)

from contextlib import ExitStack

import concourse.mybir as mybir
from concourse.masks import make_identity

F32 = mybir.dt.float32
BF16 = mybir.dt.bfloat16
U32 = mybir.dt.uint32
U8 = mybir.dt.uint8
FP8X4 = mybir.dt.float8_e4m3fn_x4
ACT = mybir.ActivationFunctionType
ALU = mybir.AluOpType

P = 128
ATOMS, C, F, G = 2048, 3, 512, 256
NT = ATOMS // P
EPS = 1e-08
FLOPS = 2 * ATOMS * C * (2 * F) * F + 2 * ATOMS * G * (2 * F)

MU_LOADS = [(0, 1), (1, 2), (2, 4), (4, 8), (8, 12), (12, 16)]
Q_LOADS = [(0, 2), (2, 4), (4, 8), (8, 16)]
H_STORES = [(0, 4), (4, 8), (8, 12), (12, 14), (14, 16)]
BANKS = {"w": 2, "v": 3, "misc": 2, "ss": 1}
DEPTH = {
    "grouped": 3,
    "codes": 6,
    "mu_w": 4,
    "sq": 8,
    "prod": 6,
    "sum01": 2,
    "mu_vw": 4,
    "root": 3,
}
VECTOR_HELPS_FROM = NT - 2
WARM_UP = 9
WARM_UP_MORE = 2


def tile_painnmixing_pa_t_kernel(tc, q, mu, W_mix, W1, b1, out_0, out_1, out_2):
    nc = tc.nc
    with ExitStack() as ctx:
        const = ctx.enter_context(tc.tile_pool(name="const", bufs=1))
        work = ctx.enter_context(tc.tile_pool(name="work", bufs=1))
        psum = ctx.enter_context(tc.psum_pool(name="psum", bufs=1))
        ctx.enter_context(tc.manual_schedule())

        q_v = q.rearrange("(p i) o k -> p i (o k)", i=NT)
        mu_v = mu.rearrange("(p i) c k -> p i c k", i=NT)
        h_v = out_0.rearrange("(p i) o g -> p i (o g)", i=NT)
        muw_v = out_1.rearrange("(p i) c f -> p i (c f)", i=NT)
        vw_v = out_2.rearrange("(p i) o f -> p i (o f)", i=NT)
        wm_v = W_mix.rearrange("(r p) k -> p r k", p=P)
        w1_v = W1.rearrange("(r p) k -> p r k", p=P)

        mu_sb = [const.tile([P, hi - lo, C, F], BF16, name="mu_sb%d" % j) for j, (lo, hi) in enumerate(MU_LOADS)]
        q_sb = [const.tile([P, hi - lo, F], BF16, name="q_sb%d" % j) for j, (lo, hi) in enumerate(Q_LOADS)]
        wm_sb = [const.tile([P, 4, F], BF16, name="wm_sb%d" % j) for j in range(2)]
        w1_sb = const.tile([P, 2, 2 * F], BF16, name="w1_sb")
        b1_row = const.tile([P, G], BF16, name="b1_row")
        ones_b = const.tile([P, P], BF16, name="ones_b")
        zer_b = const.tile([P, F], BF16, name="zer_b")
        b1_f = const.tile([P, G], F32, name="b1_f")
        ident_f = const.tile([P, P], F32, name="ident_f")
        ident_b = const.tile([P, P], BF16, name="ident_b")
        eps_t = const.tile([P, 1], F32, name="eps_t")
        first_root = const.tile([P, 1], F32, name="first_root")
        wm_g = [const.tile([P, 4, P, 4], BF16, name="wm_g%d" % j, align_bytes=64) for j in range(2)]
        wm_codes = const.tile([P, 2 * F], U32, name="wm_codes", align_bytes=64)
        wm_scales = const.tile([P, 2 * F], U8, name="wm_scales", align_bytes=64)
        w1_g = const.tile([P, 2, 2, P, 4], BF16, name="w1_g", align_bytes=64)
        w1_codes = const.tile([P, 2, G], U32, name="w1_codes", align_bytes=64)
        w1_scales = const.tile([P, 2, G], U8, name="w1_scales", align_bytes=64)
        hpre = const.tile([P, NT, G], F32, name="hpre")

        live = {}
        turn = {}

        def bank(group, shape, dtype):
            k = turn.get(group, 0)
            turn[group] = k + 1
            return psum.tile(shape, dtype, name=group + "_ps", tag="%s%d" % (group, k % BANKS[group]), bufs=1)

        def is_tile(i):
            return 0 <= i < NT

        def load_mu(j):
            lo, hi = MU_LOADS[j]
            nc.sync.dma_start(out=mu_sb[j][:], in_=mu_v[:, lo:hi, :, :])

        def load_q(j):
            lo, hi = Q_LOADS[j]
            nc.sync.dma_start(out=q_sb[j][:], in_=q_v[:, lo:hi, :])

        def mu_words(i, c):
            j = [lo <= i < hi for lo, hi in MU_LOADS].index(True)
            return mu_sb[j][:].bitcast(F32)[:, i - MU_LOADS[j][0], c, :]

        def q_words(i):
            j = [lo <= i < hi for lo, hi in Q_LOADS].index(True)
            return q_sb[j][:].bitcast(F32)[:, i - Q_LOADS[j][0], :]

        def transpose_words(dst, sources):
            for r, src in enumerate(sources):
                for u in range(2):
                    nc.tensor.transpose(dst[:, r, u, :], src[:, u * P:(u + 1) * P], ident_f[:])

        def regroup(engine, dst, src):
            if engine == "vector":
                nc.vector.tensor_copy(out=dst, in_=src.rearrange("p r u a -> p r a u"))
            else:
                nc.scalar.copy(out=dst, in_=src.rearrange("p r u a -> p r a u"))

        def transpose_inputs(i, half):
            if not is_tile(i):
                return
            dst = bank("misc", [P, 2, 2, P], F32)
            if half == 0:
                live["grouped", i] = work.tile([P, 4, P, 4], BF16, name="g", tag="g", bufs=DEPTH["grouped"], align_bytes=64)
                transpose_words(dst, [mu_words(i, 0), mu_words(i, 1)])
            else:
                transpose_words(dst, [mu_words(i, 2), q_words(i)])
            live["inputsT", i, half] = dst

        def regroup_inputs(i, half, engine="vector"):
            if not is_tile(i):
                return
            regroup(engine, live["grouped", i][:].bitcast(F32)[:, 2 * half:2 * half + 2, :, :], live["inputsT", i, half][:])

        def quantise_inputs(i):
            if not is_tile(i):
                return
            codes = work.tile([P, 4 * P], U32, name="codes", tag="codes", bufs=DEPTH["codes"], align_bytes=64)
            scales = work.tile([P, 4 * P], U8, name="scales", tag="scales", bufs=DEPTH["codes"], align_bytes=64)
            nc.vector.quantize_mx(out=codes[:].bitcast(FP8X4), scales=scales[:],
                                  in_=live["grouped", i][:].rearrange("p r a t -> p (r a t)"))
            live["codes", i] = codes
            live["scales", i] = scales

        def mix(i, c, part):
            if not is_tile(i):
                return
            dst = bank(part, [P, F], F32)
            first = 0 if part == "v" else F
            nc.tensor.matmul_mx(
                out=dst[:],
                lhsT=live["codes", i][:, c * P:(c + 1) * P].bitcast(FP8X4),
                lhsT_scale=live["scales", i][:, c * P:(c + 1) * P],
                rhs=wm_codes[:, first:first + F].bitcast(FP8X4),
                rhs_scale=wm_scales[:, first:first + F],
                start=True,
                stop=True,
            )
            live[part, i, c] = dst

        def copy_mu_w(i, c):
            if not is_tile(i):
                return
            if c == 0:
                live["mu_w", i] = work.tile([P, C, F], F32, name="wout", tag="wout", bufs=DEPTH["mu_w"])
            if i >= VECTOR_HELPS_FROM and c > 0:
                nc.vector.tensor_copy(out=live["mu_w", i][:, c, :], in_=live["w", i, c][:])
            else:
                nc.scalar.copy(out=live["mu_w", i][:, c, :], in_=live["w", i, c][:])

        def square(i, c):
            if not is_tile(i):
                return
            sq = work.tile([P, F], F32, name="sq", tag="sq", bufs=DEPTH["sq"])
            nc.scalar.activation(out=sq[:], in_=live["v", i, c][:], func=ACT.Square)
            live["sq", i, c] = sq

        def product(i, c):
            if not is_tile(i):
                return
            prod = work.tile([P, F], F32, name="prod", tag="prod", bufs=DEPTH["prod"])
            nc.vector.tensor_tensor(out=prod[:], in0=live["v", i, c][:], in1=live["mu_w", i][:, c, :], op=ALU.mult)
            live["prod", i, c] = prod

        def add_first_two_products(i):
            if not is_tile(i):
                return
            live["sum01", i] = work.tile([P, F], F32, name="acc", tag="acc", bufs=DEPTH["sum01"])
            nc.gpsimd.tensor_tensor(out=live["sum01", i][:], in0=live["prod", i, 0][:], in1=live["prod", i, 1][:], op=ALU.add)

        def add_third_product(i):
            if not is_tile(i):
                return
            live["mu_vw", i] = work.tile([P, F], F32, name="vw", tag="vw", bufs=DEPTH["mu_vw"])
            nc.gpsimd.tensor_tensor(out=live["mu_vw", i][:], in0=live["sum01", i][:], in1=live["prod", i, 2][:], op=ALU.add)

        def sum_squares(i):
            if not is_tile(i):
                return
            ss = bank("ss", [P, 4, P], F32)
            for c in range(C):
                for t in range(4):
                    nc.tensor.matmul(out=ss[:, t, :], lhsT=live["sq", i, c][:, t * P:(t + 1) * P], rhs=ident_f[:],
                                     is_transpose=True, start=(c == 0 and t == 0), stop=(c == C - 1 and t == 3))
            live["ss", i] = ss

        def root(i):
            if not is_tile(i):
                return
            vn_g = work.tile([P, P, 4], BF16, name="vn_g", tag="vn_g", bufs=DEPTH["root"], align_bytes=64)
            nc.scalar.activation(out=vn_g[:], in_=live["ss", i][:].rearrange("p t a -> p a t"), func=ACT.Sqrt,
                                 bias=eps_t[:, 0:1], scale=1.0)
            live["vn_g", i] = vn_g

        def quantise_root(i):
            if not is_tile(i):
                return
            vn_codes = work.tile([P, P], U32, name="vn_codes", tag="vn_codes", bufs=DEPTH["root"], align_bytes=64)
            vn_scales = work.tile([P, P], U8, name="vn_scales", tag="vn_scales", bufs=DEPTH["root"], align_bytes=64)
            nc.vector.quantize_mx(out=vn_codes[:].bitcast(FP8X4), scales=vn_scales[:],
                                  in_=live["vn_g", i][:].rearrange("p a t -> p (a t)"))
            live["vn_codes", i] = vn_codes
            live["vn_scales", i] = vn_scales

        def second_matmul(i):
            if not is_tile(i):
                return
            h_ps = bank("misc", [P, G], F32)
            nc.tensor.matmul_mx(out=h_ps[:], lhsT=live["codes", i][:, 3 * P:4 * P].bitcast(FP8X4),
                                lhsT_scale=live["scales", i][:, 3 * P:4 * P], rhs=w1_codes[:, 0, :].bitcast(FP8X4),
                                rhs_scale=w1_scales[:, 0, :], start=True, stop=False)
            nc.tensor.matmul_mx(out=h_ps[:], lhsT=live["vn_codes", i][:].bitcast(FP8X4),
                                lhsT_scale=live["vn_scales", i][:], rhs=w1_codes[:, 1, :].bitcast(FP8X4),
                                rhs_scale=w1_scales[:, 1, :], start=False, stop=True)
            nc.vector.tensor_tensor(out=hpre[:, i, :], in0=h_ps[:], in1=b1_f[:], op=ALU.add)

        def store_mu_w(i):
            if is_tile(i):
                nc.sync.dma_start(out=muw_v[:, i, :], in_=live["mu_w", i][:].rearrange("p c f -> p (c f)"))

        def store_mu_vw(i):
            if is_tile(i):
                nc.sync.dma_start(out=vw_v[:, i, :], in_=live["mu_vw", i][:])

        def transpose_w_mix(j, b):
            words = wm_sb[j][:].bitcast(F32)
            dst = bank("v", [P, 2, 2, P], F32)
            transpose_words(dst, [words[:, 2 * b, :], words[:, 2 * b + 1, :]])
            live["wmT", j, b] = dst

        def regroup_w_mix(j, b, engine):
            regroup(engine, wm_g[j][:].bitcast(F32)[:, 2 * b:2 * b + 2, :, :], live["wmT", j, b][:])

        def quantise_w_mix(j):
            nc.vector.quantize_mx(out=wm_codes[:, j * F:(j + 1) * F].bitcast(FP8X4),
                                  scales=wm_scales[:, j * F:(j + 1) * F],
                                  in_=wm_g[j][:].rearrange("p r a t -> p (r a t)"))

        def prepare_w1(part):
            if part == 0:
                words = w1_sb[:].bitcast(F32)
                dst = bank("misc", [P, 2, 2, P], F32)
                transpose_words(dst, [words[:, 0, 0:2 * P], words[:, 1, 0:2 * P]])
                regroup("vector", w1_g[:].bitcast(F32)[:, 0, :, :, :], dst[:])
            elif part == 1:
                dst = bank("misc", [P, 2, 4, P], BF16)
                for r in range(2):
                    for t in range(4):
                        nc.tensor.transpose(dst[:, r, t, :], w1_sb[:, r, F + t * P:F + (t + 1) * P], ident_b[:])
                nc.vector.tensor_copy(out=w1_g[:, 1, :, :, :], in_=dst[:].rearrange("p r t a -> p r a t"))
            else:
                dst = bank("misc", [P, G], F32)
                nc.tensor.matmul(out=dst[:], lhsT=ones_b[:], rhs=b1_row[:], start=True, stop=True)
                nc.vector.tensor_copy(out=b1_f[:], in_=dst[:])

        def quantise_w1():
            nc.vector.quantize_mx(out=w1_codes[:].rearrange("p j g -> p (j g)").bitcast(FP8X4),
                                  scales=w1_scales[:].rearrange("p j g -> p (j g)"),
                                  in_=w1_g[:].rearrange("p j r a t -> p (j r a t)"))

        def warm_up(n):
            for k in range(n):
                nc.tensor.matmul(out=bank("w", [P, F], F32)[:], lhsT=ones_b[:], rhs=zer_b[:], start=True, stop=True)

        nc.vector.memset(b1_row[:], 0.0)
        nc.vector.memset(ones_b[:], 1.0)
        nc.vector.memset(zer_b[:], 0.0)
        nc.sync.dma_start(out=wm_sb[0][:], in_=wm_v[:, 0:4, :])
        load_mu(0)
        load_q(0)
        nc.sync.dma_start(out=wm_sb[1][:], in_=wm_v[:, 4:8, :])
        load_mu(1)
        load_mu(2)
        load_q(1)
        nc.sync.dma_start(out=w1_sb[:], in_=w1_v)
        nc.sync.dma_start(out=b1_row[0:1, :], in_=b1.rearrange("(o g) -> o g", o=1))
        load_mu(3)
        load_q(2)
        nc.vector.memset(eps_t[:], EPS)
        make_identity(nc, ident_f[:])
        make_identity(nc, ident_b[:])
        nc.scalar.activation(out=first_root[:], in_=eps_t[:], func=ACT.Sqrt)

        warm_up(WARM_UP)
        for b in range(2):
            transpose_w_mix(0, b)
        regroup_w_mix(0, 0, "vector")
        regroup_w_mix(0, 1, "scalar")
        for half in range(2):
            transpose_inputs(0, half)
        regroup_inputs(0, 0, "vector")
        regroup_inputs(0, 1, "scalar")
        warm_up(WARM_UP_MORE)
        quantise_w_mix(0)
        quantise_inputs(0)
        for b in range(2):
            transpose_w_mix(1, b)
        regroup_w_mix(1, 0, "vector")
        regroup_w_mix(1, 1, "scalar")
        quantise_w_mix(1)
        transpose_inputs(1, 0)
        for c in range(C):
            mix(0, c, "v")
        transpose_inputs(1, 1)
        for c in range(C):
            square(0, c)
        mix(0, 0, "w")
        mix(0, 1, "w")
        regroup_inputs(1, 0)
        regroup_inputs(1, 1)
        quantise_inputs(1)
        copy_mu_w(0, 0)
        copy_mu_w(0, 1)

        for i in range(NT + 3):
            product(i - 1, 2)
            if 1 <= i <= 3:
                prepare_w1(i - 1)
            transpose_inputs(i + 2, 0)
            regroup_inputs(i + 2, 0)
            sum_squares(i - 1)
            transpose_inputs(i + 2, 1)
            if i > 0:
                square(i, 0)
                copy_mu_w(i, 0)
            product(i, 0)
            regroup_inputs(i + 2, 1)
            if i > 0:
                copy_mu_w(i, 1)
                square(i, 1)
            product(i, 1)
            add_first_two_products(i)
            add_third_product(i - 1)
            quantise_inputs(i + 2)
            if i == 2:
                quantise_w1()
            quantise_root(i - 2)
            root(i - 1)
            mix(i, 2, "w")
            if i > 0:
                mix(i, 2, "v")
            second_matmul(i - 3)
            mix(i + 1, 0, "v")
            mix(i + 1, 0, "w")
            copy_mu_w(i, 2)
            if i > 0:
                square(i, 2)
            mix(i + 1, 1, "w")
            mix(i + 1, 1, "v")
            store_mu_w(i)
            if i == 1:
                load_mu(4)
                load_q(3)
            if i == 4:
                load_mu(5)
            store_mu_vw(i - 1)

        for lo, hi in H_STORES:
            nc.scalar.activation(out=hpre[:, lo:hi, :], in_=hpre[:, lo:hi, :], func=ACT.Silu)
            nc.sync.dma_start(out=h_v[:, lo:hi, :], in_=hpre[:, lo:hi, :])
